import numpy as np
import ml_dtypes


def mxq(x, axis, fmt="e4m3"):
    dtype, down = {"e4m3": (ml_dtypes.float8_e4m3fn, 7), "e5m2": (ml_dtypes.float8_e5m2, 14)}[fmt]
    v = np.moveaxis(np.asarray(x, np.float32).astype(ml_dtypes.bfloat16).astype(np.float64), axis, -1)
    blocks = v.reshape(v.shape[:-1] + (-1, 32))
    amax = np.abs(blocks).max(-1, keepdims=True)
    byte = np.maximum(np.where(amax > 0, np.frexp(amax)[1] - 1 + 127, 0) - down, 1)
    scale = np.exp2(byte - 127.0)
    codes = (blocks / scale).astype(np.float32).astype(dtype).astype(np.float64)
    return np.moveaxis((codes * scale).reshape(v.shape), -1, axis)


WIDE = False


def mx_kscale(k):
    if not WIDE:
        return np.ones(k)
    levels = np.array([10, -10, 5, -5, 0])
    a = np.random.permutation(np.resize(levels, k // 512 * 4)).reshape(k // 512, 4)
    idx = np.arange(k)
    return np.exp2(a[idx // 512, idx % 128 // 32])


BF16 = ml_dtypes.bfloat16


def bf(x):
    return np.asarray(x, np.float32).astype(BF16)


def f64(x):
    return np.asarray(x).astype(np.float64)


B, D, C, SHOT, U, R = 2048, 512, 128, 16, 16384, 8


def setup_inputs():
    s = mx_kscale(U)
    g = np.exp2(np.round(np.log2(s.mean())))
    basis = np.random.standard_normal((R, D)) * 1.5 / np.sqrt(R * D)
    zq = np.random.standard_normal((B, R))
    zc = np.random.standard_normal((C, R))
    zu = np.random.standard_normal((U, R))
    x1 = zq @ basis + np.random.standard_normal((B, D)) / np.sqrt(D)
    x2 = (zc @ basis)[:, None, :] + np.random.standard_normal((C, SHOT, D)) / np.sqrt(D)
    x3 = zu @ basis + np.random.standard_normal((U, D)) / np.sqrt(D)
    lg = -0.5 * ((zu[:, None, :] - zc[None, :, :]) ** 2).sum(-1)
    w = np.exp(lg - lg.max(1, keepdims=True))
    w = w / w.sum(1, keepdims=True)
    return {"x1": bf(x1.reshape(B, D, 1, 1)), "x2": bf(x2), "x3": bf(x3 * (g / s)[:, None]), "w": bf(w * (s / g)[:, None])}


def reference(x1, x2, x3, w):
    x1, x2, x3, w = f64(x1), f64(x2), f64(x3), f64(w)
    b = x1.shape[0]
    q = x1.reshape(b, -1)
    n_class, shot, d = x2.shape
    weighted_unlab = mxq(w, 0, "e4m3").T @ mxq(x3, 0, "e4m3")
    denom = shot + np.sum(w, axis=0)
    proto = (np.sum(x2, axis=1) + weighted_unlab) / denom[:, None]
    q2 = np.sum(q * q, axis=-1)
    p2 = np.sum(proto * proto, axis=-1)
    cross = mxq(q, 1, "e4m3") @ mxq(proto, 1, "e4m3").T
    return -(q2[:, None] + p2[None, :] - 2.0 * cross)

@@ -1,0 +1,259 @@
+from contextlib import ExitStack
+
+import concourse.mybir as mybir
+from concourse.masks import make_identity
+
+F32 = mybir.dt.float32
+BF16 = mybir.dt.bfloat16
+U32 = mybir.dt.uint32
+U8 = mybir.dt.uint8
+FP8X4 = mybir.dt.float8_e4m3fn_x4
+ALU = mybir.AluOpType
+ACT = mybir.ActivationFunctionType
+
+P = 128
+PACK = 4
+K_PASS = P * PACK
+
+B, D, C, SHOT, U = 2048, 512, 128, 16, 16384
+PASSES = U // K_PASS
+ROUND_PASSES = 2
+ROUNDS = PASSES // ROUND_PASSES
+W_LOAD_PASSES = 8
+W_GROUP_PASSES = 4
+Q_TILES = B // P
+ONES_COLS = 32
+X2_TILES = C * SHOT // K_PASS
+X2_CLASSES = C // X2_TILES
+
+FLOPS = 2 * U * C * D + 2 * B * D * C
+
+
+def regroup(copy, grouped, rows):
+    copy(
+        out=grouped.rearrange("p (c i) j -> p c j i", i=4),
+        in_=rows.rearrange("p j (c i) -> p c j i", i=4),
+    )
+
+
+def tile_proto_metric_semi_k_kernel(tc, x1, x2, x3, w, out):
+    nc = tc.nc
+
+    x3_view = x3.rearrange("(g p j) d -> p g j d", p=P, j=PACK)
+    w_view = w.rearrange("(g p j) c -> p g j c", p=P, j=PACK)
+    x2_view = x2.rearrange("c s d -> (c s) d").rearrange("(t p e) d -> p t e d", p=P, e=PACK)
+    x1_view = x1.rearrange("(p t) d a b -> p t (d a b)", t=Q_TILES)
+    out_view = out.rearrange("(p t) c -> p t c", t=Q_TILES)
+
+    with ExitStack() as stack:
+        keep = stack.enter_context(tc.tile_pool(name="keep", bufs=1))
+        raw = stack.enter_context(tc.tile_pool(name="raw", bufs=6))
+        stage = stack.enter_context(tc.tile_pool(name="stage", bufs=4))
+        w_stage = stack.enter_context(tc.tile_pool(name="w_stage", bufs=2))
+        psum_keep = stack.enter_context(tc.psum_pool(name="psum_keep", bufs=1))
+        psum_work = stack.enter_context(tc.psum_pool(name="psum_work", bufs=2))
+        psum_cross = stack.enter_context(tc.psum_pool(name="psum_cross", bufs=4))
+
+        ident = keep.tile([P, P], F32)
+        make_identity(nc, ident[:])
+        ones = keep.tile([P, ONES_COLS], BF16)
+        nc.vector.memset(ones[:], 1.0)
+        class_of_row_f32 = keep.tile([P, X2_CLASSES], F32)
+        nc.vector.tensor_reduce(
+            out=class_of_row_f32[:],
+            in_=ident[:].rearrange("p (n e) -> p n e", e=PACK),
+            axis=mybir.AxisListType.X,
+            op=ALU.add,
+        )
+        class_of_row = keep.tile([P, X2_CLASSES], BF16)
+        nc.vector.tensor_copy(out=class_of_row[:], in_=class_of_row_f32[:])
+
+        w_raw = [
+            keep.tile([P, W_LOAD_PASSES, PACK, C], BF16, name="w_raw%d" % a)
+            for a in range(PASSES // W_LOAD_PASSES)
+        ]
+        w_codes = keep.tile([P, PASSES, C], U32, align_bytes=64)
+        w_scales = keep.tile([P, PASSES, C], U8, align_bytes=64)
+        x2_raw = keep.tile([P, X2_TILES, PACK, D], BF16)
+        q_raw = keep.tile([P, Q_TILES, D], BF16)
+        q_grouped = keep.tile([P, Q_TILES, P * PACK], BF16, align_bytes=64)
+        q_codes = keep.tile([P, Q_TILES, P], U32, align_bytes=64)
+        q_scales = keep.tile([P, Q_TILES, P], U8, align_bytes=64)
+        q2 = keep.tile([P, Q_TILES], F32)
+        out_sb = keep.tile([P, Q_TILES, C], F32)
+        sx2_perm = keep.tile([P, 2, D // 2], F32)
+
+        wu_ps = psum_keep.tile([P, D], F32)
+        den_ps = psum_keep.tile([P, D], F32)
+
+        def support_sums():
+            sx2T_ps = psum_work.tile([P, PACK, C], F32, tag="work")
+            for t in range(X2_TILES):
+                for s in range(D // P):
+                    for e in range(PACK):
+                        nc.tensor.matmul(
+                            out=sx2T_ps[:, s, t * X2_CLASSES : (t + 1) * X2_CLASSES],
+                            lhsT=x2_raw[:, t, e, s * P : (s + 1) * P],
+                            rhs=class_of_row[:],
+                            start=(e == 0),
+                            stop=(e == PACK - 1),
+                        )
+            sx2T_sb = keep.tile([P, PACK, C], F32)
+            nc.scalar.copy(out=sx2T_sb[:], in_=sx2T_ps[:])
+            sx2_ps = psum_work.tile([P, D], F32, tag="work")
+            for s in range(D // P):
+                nc.tensor.transpose(sx2_ps[:, s * P : (s + 1) * P], sx2T_sb[:, s, :], ident[:])
+            nc.scalar.copy(out=sx2_perm[:], in_=sx2_ps[:].rearrange("c (m e) -> c e m", e=2))
+
+        def query_pair(t0):
+            qT_ps = psum_work.tile([P, 2, 2, P], F32, tag="work")
+            for tt in range(2):
+                t = t0 + tt
+                sq_junk = stage.tile([P, D], BF16)
+                nc.scalar.activation(
+                    out=sq_junk[:], in_=q_raw[:, t, :], func=ACT.Square, accum_out=q2[:, t : t + 1]
+                )
+                words = q_raw[:, t, :].bitcast(F32)
+                for u in range(2):
+                    nc.tensor.transpose(qT_ps[:, tt, u, :], words[:, u * P : (u + 1) * P], ident[:])
+            nc.scalar.copy(
+                out=q_grouped[:, t0 : t0 + 2, :].bitcast(F32).rearrange("p t (i u) -> p t i u", u=2),
+                in_=qT_ps[:].rearrange("p t u i -> p t i u"),
+            )
+
+        def query_quantise(t0):
+            nc.vector.quantize_mx(
+                out=q_codes[:, t0 : t0 + 4, :].rearrange("p t i -> p (t i)").bitcast(FP8X4),
+                scales=q_scales[:, t0 : t0 + 4, :].rearrange("p t i -> p (t i)"),
+                in_=q_grouped[:, t0 : t0 + 4, :].rearrange("p t x -> p (t x)"),
+            )
+
+        for r in range(ROUNDS):
+            g0 = r * ROUND_PASSES
+            if g0 % W_LOAD_PASSES == 0:
+                a = g0 // W_LOAD_PASSES
+                nc.sync.dma_start(out=w_raw[a][:], in_=w_view[:, g0 : g0 + W_LOAD_PASSES])
+            x3_raw = raw.tile([P, ROUND_PASSES, PACK, D], BF16)
+            nc.sync.dma_start(out=x3_raw[:], in_=x3_view[:, g0 : g0 + ROUND_PASSES])
+            if r in (1, 3):
+                h = (r - 1) // 2
+                nc.sync.dma_start(out=x2_raw[:, 2 * h : 2 * h + 2], in_=x2_view[:, 2 * h : 2 * h + 2])
+            if r in (5, 7, 9, 11):
+                t0 = 4 * ((r - 5) // 2)
+                nc.sync.dma_start(out=q_raw[:, t0 : t0 + 4, :], in_=x1_view[:, t0 : t0 + 4, :])
+
+            if g0 % W_GROUP_PASSES == 0:
+                rows = w_raw[g0 // W_LOAD_PASSES][:, g0 % W_LOAD_PASSES : g0 % W_LOAD_PASSES + W_GROUP_PASSES]
+                w_grouped = w_stage.tile([P, W_GROUP_PASSES, C, PACK], BF16, align_bytes=64)
+                nc.vector.tensor_copy(
+                    out=w_grouped[:].rearrange("p g (c i) j -> p g c j i", i=4),
+                    in_=rows.rearrange("p g j (c i) -> p g c j i", i=4),
+                )
+                nc.vector.quantize_mx(
+                    out=w_codes[:, g0 : g0 + W_GROUP_PASSES, :].rearrange("p g c -> p (g c)").bitcast(FP8X4),
+                    scales=w_scales[:, g0 : g0 + W_GROUP_PASSES, :].rearrange("p g c -> p (g c)"),
+                    in_=w_grouped[:].rearrange("p g c j -> p (g c j)"),
+                )
+                for g in range(g0, g0 + W_GROUP_PASSES):
+                    for j in range(PACK):
+                        nc.tensor.matmul(
+                            out=den_ps[:, 0:ONES_COLS],
+                            lhsT=w_raw[g // W_LOAD_PASSES][:, g % W_LOAD_PASSES, j, :],
+                            rhs=ones[:],
+                            start=(g == 0 and j == 0),
+                            stop=(g == PASSES - 1 and j == PACK - 1),
+                        )
+
+            for k in range(ROUND_PASSES):
+                g = g0 + k
+                x3_grouped = stage.tile([P, D, PACK], BF16, align_bytes=64)
+                regroup(nc.vector.tensor_copy if k == 0 else nc.scalar.copy, x3_grouped[:], x3_raw[:, k])
+                x3_codes = stage.tile([P, D], U32, align_bytes=64)
+                x3_scales = stage.tile([P, D], U8, align_bytes=64)
+                nc.vector.quantize_mx(
+                    out=x3_codes[:].bitcast(FP8X4),
+                    scales=x3_scales[:],
+                    in_=x3_grouped[:].rearrange("p d j -> p (d j)"),
+                )
+                nc.tensor.matmul_mx(
+                    out=wu_ps[:],
+                    lhsT=w_codes[:, g, :].bitcast(FP8X4),
+                    lhsT_scale=w_scales[:, g, :],
+                    rhs=x3_codes[:].bitcast(FP8X4),
+                    rhs_scale=x3_scales[:],
+                    start=(g == 0),
+                    stop=(g == PASSES - 1),
+                )
+
+            if r == 4:
+                support_sums()
+            if r in (6, 8, 10, 12):
+                t0 = 4 * ((r - 6) // 2)
+                query_pair(t0)
+                query_pair(t0 + 2)
+                query_quantise(t0)
+
+        denom = keep.tile([P, 1], F32)
+        nc.vector.tensor_scalar_add(out=denom[:], in0=den_ps[:, 0:1], scalar1=float(SHOT))
+        recip = keep.tile([P, 1], F32)
+        nc.vector.reciprocal(out=recip[:], in_=denom[:])
+        sx2_scaled = keep.tile([P, 2, D // 2], F32)
+        nc.vector.tensor_scalar_mul(out=sx2_scaled[:], in0=sx2_perm[:], scalar1=recip[:, 0:1])
+        proto = keep.tile([P, 2, D // 2], F32)
+        nc.vector.scalar_tensor_tensor(
+            out=proto[:],
+            in0=wu_ps[:].rearrange("c (m e) -> c e m", e=2),
+            scalar=recip[:, 0:1],
+            in1=sx2_scaled[:],
+            op0=ALU.mult,
+            op1=ALU.add,
+        )
+        p2 = keep.tile([P, 1], F32)
+        proto_sq = keep.tile([P, 2, D // 2], F32)
+        nc.scalar.activation(out=proto_sq[:], in_=proto[:], func=ACT.Square, accum_out=p2[:, 0:1])
+        p2_ps = psum_work.tile([P, D], F32, tag="work")
+        nc.tensor.matmul(
+            out=p2_ps[:, 0:C], lhsT=p2[:, 0:1].to_broadcast([P, P]), rhs=ident[:], start=True, stop=True
+        )
+        p2_rows = keep.tile([P, C], F32)
+        nc.scalar.copy(out=p2_rows[:], in_=p2_ps[:, 0:C])
+
+        protoT_ps = psum_work.tile([P, PACK, C], F32, tag="work")
+        for u in range(2):
+            for e in range(2):
+                nc.tensor.transpose(protoT_ps[:, 2 * u + e, :], proto[:, e, u * P : (u + 1) * P], ident[:])
+        p_grouped = keep.tile([P, C, PACK], BF16, align_bytes=64)
+        nc.vector.tensor_scalar_mul(
+            out=p_grouped[:], in0=protoT_ps[:].rearrange("p t c -> p c t"), scalar1=2.0
+        )
+        p_codes = keep.tile([P, C], U32, align_bytes=64)
+        p_scales = keep.tile([P, C], U8, align_bytes=64)
+        nc.vector.quantize_mx(
+            out=p_codes[:].bitcast(FP8X4),
+            scales=p_scales[:],
+            in_=p_grouped[:].rearrange("p c t -> p (c t)"),
+        )
+
+        for t0 in range(0, Q_TILES, 4):
+            cross_ps = psum_cross.tile([P, 4, C], F32)
+            for tt in range(4):
+                nc.tensor.matmul_mx(
+                    out=cross_ps[:, tt, :],
+                    lhsT=q_codes[:, t0 + tt, :].bitcast(FP8X4),
+                    lhsT_scale=q_scales[:, t0 + tt, :],
+                    rhs=p_codes[:].bitcast(FP8X4),
+                    rhs_scale=p_scales[:],
+                    start=True,
+                    stop=True,
+                )
+            for tt in range(4):
+                t = t0 + tt
+                nc.vector.scalar_tensor_tensor(
+                    out=out_sb[:, t, :],
+                    in0=cross_ps[:, tt, :],
+                    scalar=q2[:, t : t + 1],
+                    in1=p2_rows[:],
+                    op0=ALU.subtract,
+                    op1=ALU.subtract,
+                )
+            nc.sync.dma_start(out=out_view[:, t0 : t0 + 4, :], in_=out_sb[:, t0 : t0 + 4, :])

@@ -19,12 +19,17 @@ B, D, C, SHOT, U = 2048, 512, 128, 16, 16384
 PASSES = U // K_PASS
 ROUND_PASSES = 2
 ROUNDS = PASSES // ROUND_PASSES
-W_LOAD_PASSES = 8
+RAW_BUFS = 6
 W_GROUP_PASSES = 4
+W_GROUPS = PASSES // W_GROUP_PASSES
 Q_TILES = B // P
+QUARTER = Q_TILES // 4
+EARLY_QUARTERS = 3
 ONES_COLS = 32
 X2_TILES = C * SHOT // K_PASS
 X2_CLASSES = C // X2_TILES
+SHARED_VECTOR_COLS = 336
+SCALAR_BANK = 1
 
 FLOPS = 2 * U * C * D + 2 * B * D * C
 
@@ -41,18 +46,18 @@ def tile_proto_metric_semi_k_kernel(tc, x1, x2, x3, w, out):
 
     x3_view = x3.rearrange("(g p j) d -> p g j d", p=P, j=PACK)
     w_view = w.rearrange("(g p j) c -> p g j c", p=P, j=PACK)
-    x2_view = x2.rearrange("c s d -> (c s) d").rearrange("(t p e) d -> p t e d", p=P, e=PACK)
+    x2_view = x2.rearrange("c s d -> (c s) d").rearrange("(k p e) d -> p k e d", p=P, e=PACK)
     x1_view = x1.rearrange("(p t) d a b -> p t (d a b)", t=Q_TILES)
     out_view = out.rearrange("(p t) c -> p t c", t=Q_TILES)
 
     with ExitStack() as stack:
         keep = stack.enter_context(tc.tile_pool(name="keep", bufs=1))
-        raw = stack.enter_context(tc.tile_pool(name="raw", bufs=6))
+        raw = stack.enter_context(tc.tile_pool(name="raw", bufs=RAW_BUFS))
         stage = stack.enter_context(tc.tile_pool(name="stage", bufs=4))
         w_stage = stack.enter_context(tc.tile_pool(name="w_stage", bufs=2))
         psum_keep = stack.enter_context(tc.psum_pool(name="psum_keep", bufs=1))
-        psum_work = stack.enter_context(tc.psum_pool(name="psum_work", bufs=2))
-        psum_cross = stack.enter_context(tc.psum_pool(name="psum_cross", bufs=4))
+        psum_work = stack.enter_context(tc.psum_pool(name="psum_work", bufs=5))
+        stack.enter_context(tc.manual_schedule())
 
         ident = keep.tile([P, P], F32)
         make_identity(nc, ident[:])
@@ -68,10 +73,7 @@ def tile_proto_metric_semi_k_kernel(tc, x1, x2, x3, w, out):
         class_of_row = keep.tile([P, X2_CLASSES], BF16)
         nc.vector.tensor_copy(out=class_of_row[:], in_=class_of_row_f32[:])
 
-        w_raw = [
-            keep.tile([P, W_LOAD_PASSES, PACK, C], BF16, name="w_raw%d" % a)
-            for a in range(PASSES // W_LOAD_PASSES)
-        ]
+        w_raw = [keep.tile([P, W_GROUP_PASSES, PACK, C], BF16, name="w_raw%d" % a) for a in range(W_GROUPS)]
         w_codes = keep.tile([P, PASSES, C], U32, align_bytes=64)
         w_scales = keep.tile([P, PASSES, C], U8, align_bytes=64)
         x2_raw = keep.tile([P, X2_TILES, PACK, D], BF16)
@@ -81,124 +83,213 @@ def tile_proto_metric_semi_k_kernel(tc, x1, x2, x3, w, out):
         q_scales = keep.tile([P, Q_TILES, P], U8, align_bytes=64)
         q2 = keep.tile([P, Q_TILES], F32)
         out_sb = keep.tile([P, Q_TILES, C], F32)
-        sx2_perm = keep.tile([P, 2, D // 2], F32)
-
         wu_ps = psum_keep.tile([P, D], F32)
         den_ps = psum_keep.tile([P, D], F32)
+        sx2T_ps = psum_keep.tile([P, D // P, C], F32)
 
-        def support_sums():
-            sx2T_ps = psum_work.tile([P, PACK, C], F32, tag="work")
-            for t in range(X2_TILES):
-                for s in range(D // P):
-                    for e in range(PACK):
-                        nc.tensor.matmul(
-                            out=sx2T_ps[:, s, t * X2_CLASSES : (t + 1) * X2_CLASSES],
-                            lhsT=x2_raw[:, t, e, s * P : (s + 1) * P],
-                            rhs=class_of_row[:],
-                            start=(e == 0),
-                            stop=(e == PACK - 1),
-                        )
-            sx2T_sb = keep.tile([P, PACK, C], F32)
-            nc.scalar.copy(out=sx2T_sb[:], in_=sx2T_ps[:])
-            sx2_ps = psum_work.tile([P, D], F32, tag="work")
-            for s in range(D // P):
-                nc.tensor.transpose(sx2_ps[:, s * P : (s + 1) * P], sx2T_sb[:, s, :], ident[:])
-            nc.scalar.copy(out=sx2_perm[:], in_=sx2_ps[:].rearrange("c (m e) -> c e m", e=2))
+        x3_raw, x3_grouped, x3_codes, x3_scales, w_grouped, qT_ps = {}, {}, {}, {}, {}, {}
 
-        def query_pair(t0):
-            qT_ps = psum_work.tile([P, 2, 2, P], F32, tag="work")
+        def load_w(a):
+            g0 = a * W_GROUP_PASSES
+            nc.sync.dma_start(out=w_raw[a][:], in_=w_view[:, g0 : g0 + W_GROUP_PASSES])
+
+        def load_queries(quarter):
+            t0 = quarter * QUARTER
+            nc.sync.dma_start(out=q_raw[:, t0 : t0 + QUARTER, :], in_=x1_view[:, t0 : t0 + QUARTER, :])
+
+        def load_round(r):
+            g0 = r * ROUND_PASSES
+            x3_raw[r] = raw.tile([P, ROUND_PASSES, PACK, D], BF16, name="x3_raw")
+            if r in (0, ROUNDS - 1):
+                nc.sync.dma_start(out=x3_raw[r][:, 0:1], in_=x3_view[:, g0 : g0 + 1])
+                if r == 0:
+                    load_w(0)
+                nc.sync.dma_start(out=x3_raw[r][:, 1:2], in_=x3_view[:, g0 + 1 : g0 + 2])
+            else:
+                nc.sync.dma_start(out=x3_raw[r][:], in_=x3_view[:, g0 : g0 + ROUND_PASSES])
+            if r % 2 == 1 and (r + 1) // 2 < W_GROUPS:
+                load_w((r + 1) // 2)
+            if r % 2 == 0:
+                piece = r // 2
+                if piece < EARLY_QUARTERS:
+                    load_queries(piece)
+                elif piece < EARLY_QUARTERS + X2_TILES:
+                    k = piece - EARLY_QUARTERS
+                    nc.sync.dma_start(out=x2_raw[:, k], in_=x2_view[:, k])
+            if r == ROUNDS - 1:
+                load_queries(EARLY_QUARTERS)
+
+        def regroup_pass(g, vector_cols):
+            rows = x3_raw[g // ROUND_PASSES][:, g % ROUND_PASSES]
+            x3_grouped[g] = stage.tile([P, D, PACK], BF16, align_bytes=64, name="x3_grouped")
+            if vector_cols > 0:
+                regroup(nc.vector.tensor_copy, x3_grouped[g][:, 0:vector_cols, :], rows[:, :, 0:vector_cols])
+            if vector_cols < D:
+                regroup(nc.scalar.copy, x3_grouped[g][:, vector_cols:D, :], rows[:, :, vector_cols:D])
+
+        def quantise_pass(g):
+            x3_codes[g] = stage.tile([P, D], U32, align_bytes=64, name="x3_codes")
+            x3_scales[g] = stage.tile([P, D], U8, align_bytes=64, name="x3_scales")
+            nc.vector.quantize_mx(
+                out=x3_codes[g][:].bitcast(FP8X4),
+                scales=x3_scales[g][:],
+                in_=x3_grouped[g][:].rearrange("p d j -> p (d j)"),
+            )
+
+        def multiply_pass(g):
+            nc.tensor.matmul_mx(
+                out=wu_ps[:],
+                lhsT=w_codes[:, g, :].bitcast(FP8X4),
+                lhsT_scale=w_scales[:, g, :],
+                rhs=x3_codes[g][:].bitcast(FP8X4),
+                rhs_scale=x3_scales[g][:],
+                start=(g == 0),
+                stop=(g == PASSES - 1),
+            )
+
+        def regroup_w(a):
+            w_grouped[a] = w_stage.tile([P, W_GROUP_PASSES, C, PACK], BF16, align_bytes=64, name="w_grouped")
+            nc.vector.tensor_copy(
+                out=w_grouped[a][:].rearrange("p g (c i) j -> p g c j i", i=4),
+                in_=w_raw[a][:].rearrange("p g j (c i) -> p g c j i", i=4),
+            )
+
+        def quantise_w(a):
+            g0 = a * W_GROUP_PASSES
+            nc.vector.quantize_mx(
+                out=w_codes[:, g0 : g0 + W_GROUP_PASSES, :].rearrange("p g c -> p (g c)").bitcast(FP8X4),
+                scales=w_scales[:, g0 : g0 + W_GROUP_PASSES, :].rearrange("p g c -> p (g c)"),
+                in_=w_grouped[a][:].rearrange("p g c j -> p (g c j)"),
+            )
+
+        def sum_w(a):
+            for g in range(W_GROUP_PASSES):
+                for j in range(PACK):
+                    nc.tensor.matmul(
+                        out=den_ps[:, 0:ONES_COLS],
+                        lhsT=w_raw[a][:, g, j, :],
+                        rhs=ones[:],
+                        start=(a == 0 and g == 0 and j == 0),
+                        stop=(a == W_GROUPS - 1 and g == W_GROUP_PASSES - 1 and j == PACK - 1),
+                    )
+
+        def query_norm(t):
+            sq_junk = stage.tile([P, D], BF16)
+            nc.scalar.activation(
+                out=sq_junk[:], in_=q_raw[:, t, :], func=ACT.Square, accum_out=q2[:, t : t + 1]
+            )
+
+        def query_transposes(t0):
+            qT_ps[t0] = psum_work.tile([P, 2, 2, P], F32, name="qT_ps", tag="work")
             for tt in range(2):
-                t = t0 + tt
-                sq_junk = stage.tile([P, D], BF16)
-                nc.scalar.activation(
-                    out=sq_junk[:], in_=q_raw[:, t, :], func=ACT.Square, accum_out=q2[:, t : t + 1]
-                )
-                words = q_raw[:, t, :].bitcast(F32)
+                words = q_raw[:, t0 + tt, :].bitcast(F32)
                 for u in range(2):
-                    nc.tensor.transpose(qT_ps[:, tt, u, :], words[:, u * P : (u + 1) * P], ident[:])
-            nc.scalar.copy(
+                    nc.tensor.transpose(qT_ps[t0][:, tt, u, :], words[:, u * P : (u + 1) * P], ident[:])
+
+        def query_regroup(copy, t0):
+            copy(
                 out=q_grouped[:, t0 : t0 + 2, :].bitcast(F32).rearrange("p t (i u) -> p t i u", u=2),
-                in_=qT_ps[:].rearrange("p t u i -> p t i u"),
+                in_=qT_ps[t0][:].rearrange("p t u i -> p t i u"),
             )
 
         def query_quantise(t0):
             nc.vector.quantize_mx(
-                out=q_codes[:, t0 : t0 + 4, :].rearrange("p t i -> p (t i)").bitcast(FP8X4),
-                scales=q_scales[:, t0 : t0 + 4, :].rearrange("p t i -> p (t i)"),
-                in_=q_grouped[:, t0 : t0 + 4, :].rearrange("p t x -> p (t x)"),
+                out=q_codes[:, t0 : t0 + QUARTER, :].rearrange("p t i -> p (t i)").bitcast(FP8X4),
+                scales=q_scales[:, t0 : t0 + QUARTER, :].rearrange("p t i -> p (t i)"),
+                in_=q_grouped[:, t0 : t0 + QUARTER, :].rearrange("p t x -> p (t x)"),
             )
 
-        for r in range(ROUNDS):
-            g0 = r * ROUND_PASSES
-            if g0 % W_LOAD_PASSES == 0:
-                a = g0 // W_LOAD_PASSES
-                nc.sync.dma_start(out=w_raw[a][:], in_=w_view[:, g0 : g0 + W_LOAD_PASSES])
-            x3_raw = raw.tile([P, ROUND_PASSES, PACK, D], BF16)
-            nc.sync.dma_start(out=x3_raw[:], in_=x3_view[:, g0 : g0 + ROUND_PASSES])
-            if r in (1, 3):
-                h = (r - 1) // 2
-                nc.sync.dma_start(out=x2_raw[:, 2 * h : 2 * h + 2], in_=x2_view[:, 2 * h : 2 * h + 2])
-            if r in (5, 7, 9, 11):
-                t0 = 4 * ((r - 5) // 2)
-                nc.sync.dma_start(out=q_raw[:, t0 : t0 + 4, :], in_=x1_view[:, t0 : t0 + 4, :])
+        def support_tile(k):
+            for s in range(D // P):
+                for e in range(PACK):
+                    nc.tensor.matmul(
+                        out=sx2T_ps[:, s, k * X2_CLASSES : (k + 1) * X2_CLASSES],
+                        lhsT=x2_raw[:, k, e, s * P : (s + 1) * P],
+                        rhs=class_of_row[:],
+                        start=(e == 0),
+                        stop=(e == PACK - 1),
+                    )
 
-            if g0 % W_GROUP_PASSES == 0:
-                rows = w_raw[g0 // W_LOAD_PASSES][:, g0 % W_LOAD_PASSES : g0 % W_LOAD_PASSES + W_GROUP_PASSES]
-                w_grouped = w_stage.tile([P, W_GROUP_PASSES, C, PACK], BF16, align_bytes=64)
-                nc.vector.tensor_copy(
-                    out=w_grouped[:].rearrange("p g (c i) j -> p g c j i", i=4),
-                    in_=rows.rearrange("p g j (c i) -> p g c j i", i=4),
-                )
-                nc.vector.quantize_mx(
-                    out=w_codes[:, g0 : g0 + W_GROUP_PASSES, :].rearrange("p g c -> p (g c)").bitcast(FP8X4),
-                    scales=w_scales[:, g0 : g0 + W_GROUP_PASSES, :].rearrange("p g c -> p (g c)"),
-                    in_=w_grouped[:].rearrange("p g c j -> p (g c j)"),
-                )
-                for g in range(g0, g0 + W_GROUP_PASSES):
-                    for j in range(PACK):
-                        nc.tensor.matmul(
-                            out=den_ps[:, 0:ONES_COLS],
-                            lhsT=w_raw[g // W_LOAD_PASSES][:, g % W_LOAD_PASSES, j, :],
-                            rhs=ones[:],
-                            start=(g == 0 and j == 0),
-                            stop=(g == PASSES - 1 and j == PACK - 1),
-                        )
-
-            for k in range(ROUND_PASSES):
-                g = g0 + k
-                x3_grouped = stage.tile([P, D, PACK], BF16, align_bytes=64)
-                regroup(nc.vector.tensor_copy if k == 0 else nc.scalar.copy, x3_grouped[:], x3_raw[:, k])
-                x3_codes = stage.tile([P, D], U32, align_bytes=64)
-                x3_scales = stage.tile([P, D], U8, align_bytes=64)
-                nc.vector.quantize_mx(
-                    out=x3_codes[:].bitcast(FP8X4),
-                    scales=x3_scales[:],
-                    in_=x3_grouped[:].rearrange("p d j -> p (d j)"),
-                )
-                nc.tensor.matmul_mx(
-                    out=wu_ps[:],
-                    lhsT=w_codes[:, g, :].bitcast(FP8X4),
-                    lhsT_scale=w_scales[:, g, :],
-                    rhs=x3_codes[:].bitcast(FP8X4),
-                    rhs_scale=x3_scales[:],
-                    start=(g == 0),
-                    stop=(g == PASSES - 1),
-                )
-
-            if r == 4:
-                support_sums()
-            if r in (6, 8, 10, 12):
-                t0 = 4 * ((r - 6) // 2)
-                query_pair(t0)
-                query_pair(t0 + 2)
-                query_quantise(t0)
-
-        denom = keep.tile([P, 1], F32)
-        nc.vector.tensor_scalar_add(out=denom[:], in0=den_ps[:, 0:1], scalar1=float(SHOT))
         recip = keep.tile([P, 1], F32)
-        nc.vector.reciprocal(out=recip[:], in_=denom[:])
         sx2_scaled = keep.tile([P, 2, D // 2], F32)
-        nc.vector.tensor_scalar_mul(out=sx2_scaled[:], in0=sx2_perm[:], scalar1=recip[:, 0:1])
+
+        def finish_denominator():
+            denom = keep.tile([P, 1], F32)
+            nc.vector.tensor_scalar_add(out=denom[:], in0=den_ps[:, 0:1], scalar1=float(SHOT))
+            nc.vector.reciprocal(out=recip[:], in_=denom[:])
+
+        def transpose_support_sums():
+            sx2T_sb = keep.tile([P, D // P, C], F32)
+            nc.scalar.copy(out=sx2T_sb[:], in_=sx2T_ps[:])
+            sx2_ps = psum_work.tile([P, D], F32, tag="work")
+            for s in range(D // P):
+                nc.tensor.transpose(sx2_ps[:, s * P : (s + 1) * P], sx2T_sb[:, s, :], ident[:])
+            return sx2_ps
+
+        def scale_support_sums(sx2_ps):
+            nc.scalar.activation(
+                out=sx2_scaled[:],
+                in_=sx2_ps[:].rearrange("c (m e) -> c e m", e=2),
+                func=ACT.Copy,
+                scale=recip[:, 0:1],
+            )
+
+        for r in range(RAW_BUFS):
+            load_round(r)
+
+        early_tiles = EARLY_QUARTERS * QUARTER
+        last_support_round = 2 * (EARLY_QUARTERS + X2_TILES) - 1
+        for r in range(ROUNDS - 1):
+            t = r - 1
+            if r == last_support_round + 1:
+                sx2_ps = transpose_support_sums()
+            if 0 <= t < early_tiles and t % 2 == 1:
+                query_transposes(t - 1)
+            regroup_pass(2 * r, D)
+            regroup_pass(2 * r + 1, 0)
+            if r + RAW_BUFS < ROUNDS:
+                load_round(r + RAW_BUFS)
+            if r > 0:
+                quantise_pass(2 * r - 1)
+                multiply_pass(2 * r - 1)
+            a = (r + 1) // 2
+            prepares_w = (r == 0 or r % 2 == 1) and a < W_GROUPS
+            if prepares_w:
+                regroup_w(a)
+            quantise_pass(2 * r)
+            if prepares_w:
+                quantise_w(a)
+                sum_w(a)
+            multiply_pass(2 * r)
+            if 0 <= t - 1 < early_tiles and (t - 1) % QUARTER == QUARTER - 1:
+                query_quantise(t - QUARTER)
+            if 0 <= t < early_tiles:
+                query_norm(t)
+                if t % 2 == 1:
+                    query_regroup(nc.scalar.copy, t - 1)
+            k = (r - 1) // 2 - EARLY_QUARTERS
+            if r % 2 == 1 and 0 <= k < X2_TILES:
+                support_tile(k)
+            if r == last_support_round:
+                finish_denominator()
+            if r == last_support_round + 1:
+                scale_support_sums(sx2_ps)
+
+        late = EARLY_QUARTERS * QUARTER
+        regroup_pass(PASSES - 2, SHARED_VECTOR_COLS)
+        quantise_pass(PASSES - 3)
+        multiply_pass(PASSES - 3)
+        regroup_pass(PASSES - 1, SHARED_VECTOR_COLS)
+        quantise_pass(PASSES - 2)
+        multiply_pass(PASSES - 2)
+        query_transposes(late)
+        query_transposes(late + 2)
+        quantise_pass(PASSES - 1)
+        multiply_pass(PASSES - 1)
+        query_norm(late)
+        query_norm(late + 1)
+        query_regroup(nc.vector.tensor_copy, late)
+
         proto = keep.tile([P, 2, D // 2], F32)
         nc.vector.scalar_tensor_tensor(
             out=proto[:],
@@ -211,17 +302,21 @@ def tile_proto_metric_semi_k_kernel(tc, x1, x2, x3, w, out):
         p2 = keep.tile([P, 1], F32)
         proto_sq = keep.tile([P, 2, D // 2], F32)
         nc.scalar.activation(out=proto_sq[:], in_=proto[:], func=ACT.Square, accum_out=p2[:, 0:1])
-        p2_ps = psum_work.tile([P, D], F32, tag="work")
-        nc.tensor.matmul(
-            out=p2_ps[:, 0:C], lhsT=p2[:, 0:1].to_broadcast([P, P]), rhs=ident[:], start=True, stop=True
-        )
-        p2_rows = keep.tile([P, C], F32)
-        nc.scalar.copy(out=p2_rows[:], in_=p2_ps[:, 0:C])
+        query_norm(late + 2)
+        query_regroup(nc.vector.tensor_copy, late + 2)
 
         protoT_ps = psum_work.tile([P, PACK, C], F32, tag="work")
         for u in range(2):
             for e in range(2):
                 nc.tensor.transpose(protoT_ps[:, 2 * u + e, :], proto[:, e, u * P : (u + 1) * P], ident[:])
+        p2_ps = psum_work.tile([P, D], F32, tag="work")
+        nc.tensor.matmul(
+            out=p2_ps[:, 0:C], lhsT=p2[:, 0:1].to_broadcast([P, P]), rhs=ident[:], start=True, stop=True
+        )
+        neg_p2_rows = keep.tile([P, C], F32)
+        nc.scalar.mul(out=neg_p2_rows[:], in_=p2_ps[:, 0:C], mul=-1.0)
+        query_norm(late + 3)
+
         p_grouped = keep.tile([P, C, PACK], BF16, align_bytes=64)
         nc.vector.tensor_scalar_mul(
             out=p_grouped[:], in0=protoT_ps[:].rearrange("p t c -> p c t"), scalar1=2.0
@@ -233,27 +328,47 @@ def tile_proto_metric_semi_k_kernel(tc, x1, x2, x3, w, out):
             scales=p_scales[:],
             in_=p_grouped[:].rearrange("p c t -> p (c t)"),
         )
+        query_quantise(late)
 
-        for t0 in range(0, Q_TILES, 4):
-            cross_ps = psum_cross.tile([P, 4, C], F32)
-            for tt in range(4):
+        cross_ps = [psum_work.tile([P, QUARTER, C], F32, name="cross_ps", tag="work") for b in range(4)]
+        for b in range(4):
+            for tt in range(QUARTER):
                 nc.tensor.matmul_mx(
-                    out=cross_ps[:, tt, :],
-                    lhsT=q_codes[:, t0 + tt, :].bitcast(FP8X4),
-                    lhsT_scale=q_scales[:, t0 + tt, :],
+                    out=cross_ps[b][:, tt, :],
+                    lhsT=q_codes[:, b * QUARTER + tt, :].bitcast(FP8X4),
+                    lhsT_scale=q_scales[:, b * QUARTER + tt, :],
                     rhs=p_codes[:].bitcast(FP8X4),
                     rhs_scale=p_scales[:],
                     start=True,
                     stop=True,
                 )
-            for tt in range(4):
-                t = t0 + tt
-                nc.vector.scalar_tensor_tensor(
-                    out=out_sb[:, t, :],
-                    in0=cross_ps[:, tt, :],
-                    scalar=q2[:, t : t + 1],
-                    in1=p2_rows[:],
-                    op0=ALU.subtract,
-                    op1=ALU.subtract,
-                )
-            nc.sync.dma_start(out=out_view[:, t0 : t0 + 4, :], in_=out_sb[:, t0 : t0 + 4, :])
+
+        def finish_bank(b):
+            for tt in range(QUARTER):
+                t = b * QUARTER + tt
+                if b == SCALAR_BANK:
+                    q2_minus_cross = stage.tile([P, C], F32)
+                    nc.scalar.activation(
+                        out=q2_minus_cross[:],
+                        in_=cross_ps[b][:, tt, :],
+                        func=ACT.Identity,
+                        bias=q2[:, t : t + 1],
+                        scale=-1.0,
+                    )
+                    nc.gpsimd.tensor_tensor(
+                        out=out_sb[:, t, :], in0=neg_p2_rows[:], in1=q2_minus_cross[:], op=ALU.subtract
+                    )
+                else:
+                    nc.vector.scalar_tensor_tensor(
+                        out=out_sb[:, t, :],
+                        in0=cross_ps[b][:, tt, :],
+                        scalar=q2[:, t : t + 1],
+                        in1=neg_p2_rows[:],
+                        op0=ALU.subtract,
+                        op1=ALU.add,
+                    )
+            t0 = b * QUARTER
+            nc.sync.dma_start(out=out_view[:, t0 : t0 + QUARTER, :], in_=out_sb[:, t0 : t0 + QUARTER, :])
+
+        for b in (0, 2, SCALAR_BANK, 3):
+            finish_bank(b)

@@ -261,8 +261,6 @@ def tile_proto_metric_semi_k_kernel(tc, x1, x2, x3, w, out):
                 quantise_w(a)
                 sum_w(a)
             multiply_pass(2 * r)
-            if 0 <= t - 1 < early_tiles and (t - 1) % QUARTER == QUARTER - 1:
-                query_quantise(t - QUARTER)
             if 0 <= t < early_tiles:
                 query_norm(t)
                 if t % 2 == 1:
@@ -282,13 +280,14 @@ def tile_proto_metric_semi_k_kernel(tc, x1, x2, x3, w, out):
         regroup_pass(PASSES - 1, SHARED_VECTOR_COLS)
         quantise_pass(PASSES - 2)
         multiply_pass(PASSES - 2)
-        query_transposes(late)
-        query_transposes(late + 2)
         quantise_pass(PASSES - 1)
         multiply_pass(PASSES - 1)
+        query_transposes(late)
+        query_transposes(late + 2)
         query_norm(late)
         query_norm(late + 1)
-        query_regroup(nc.vector.tensor_copy, late)
+        query_quantise(0)
+        query_quantise(QUARTER)
 
         proto = keep.tile([P, 2, D // 2], F32)
         nc.vector.scalar_tensor_tensor(
@@ -303,7 +302,8 @@ def tile_proto_metric_semi_k_kernel(tc, x1, x2, x3, w, out):
         proto_sq = keep.tile([P, 2, D // 2], F32)
         nc.scalar.activation(out=proto_sq[:], in_=proto[:], func=ACT.Square, accum_out=p2[:, 0:1])
         query_norm(late + 2)
-        query_regroup(nc.vector.tensor_copy, late + 2)
+        query_quantise(2 * QUARTER)
+        query_regroup(nc.vector.tensor_copy, late)
 
         protoT_ps = psum_work.tile([P, PACK, C], F32, tag="work")
         for u in range(2):
@@ -328,6 +328,7 @@ def tile_proto_metric_semi_k_kernel(tc, x1, x2, x3, w, out):
             scales=p_scales[:],
             in_=p_grouped[:].rearrange("p c t -> p (c t)"),
         )
+        query_regroup(nc.vector.tensor_copy, late + 2)
         query_quantise(late)
 
         cross_ps = [psum_work.tile([P, QUARTER, C], F32, name="cross_ps", tag="work") for b in range(4)]

@@ -24,7 +24,7 @@ W_GROUP_PASSES = 4
 W_GROUPS = PASSES // W_GROUP_PASSES
 Q_TILES = B // P
 QUARTER = Q_TILES // 4
-EARLY_QUARTERS = 3
+EARLY_QUARTERS = 2
 ONES_COLS = 32
 X2_TILES = C * SHOT // K_PASS
 X2_CLASSES = C // X2_TILES
@@ -117,7 +117,8 @@ def tile_proto_metric_semi_k_kernel(tc, x1, x2, x3, w, out):
                     k = piece - EARLY_QUARTERS
                     nc.sync.dma_start(out=x2_raw[:, k], in_=x2_view[:, k])
             if r == ROUNDS - 1:
-                load_queries(EARLY_QUARTERS)
+                for quarter in range(EARLY_QUARTERS, Q_TILES // QUARTER):
+                    load_queries(quarter)
 
         def regroup_pass(g, vector_cols):
             rows = x3_raw[g // ROUND_PASSES][:, g % ROUND_PASSES]
@@ -239,6 +240,7 @@ def tile_proto_metric_semi_k_kernel(tc, x1, x2, x3, w, out):
 
         early_tiles = EARLY_QUARTERS * QUARTER
         last_support_round = 2 * (EARLY_QUARTERS + X2_TILES) - 1
+        last_w_round = 2 * (W_GROUPS - 1) - 1
         for r in range(ROUNDS - 1):
             t = r - 1
             if r == last_support_round + 1:
@@ -268,9 +270,9 @@ def tile_proto_metric_semi_k_kernel(tc, x1, x2, x3, w, out):
             k = (r - 1) // 2 - EARLY_QUARTERS
             if r % 2 == 1 and 0 <= k < X2_TILES:
                 support_tile(k)
-            if r == last_support_round:
+            if r == last_w_round:
                 finish_denominator()
-            if r == last_support_round + 1:
+            if r == last_w_round + 1:
                 scale_support_sums(sx2_ps)
 
         late = EARLY_QUARTERS * QUARTER
@@ -284,38 +286,41 @@ def tile_proto_metric_semi_k_kernel(tc, x1, x2, x3, w, out):
         multiply_pass(PASSES - 1)
         query_transposes(late)
         query_transposes(late + 2)
-        query_norm(late)
-        query_norm(late + 1)
+        for t in range(late, late + QUARTER):
+            query_norm(t)
         query_quantise(0)
         query_quantise(QUARTER)
 
         proto = keep.tile([P, 2, D // 2], F32)
-        nc.vector.scalar_tensor_tensor(
-            out=proto[:],
-            in0=wu_ps[:].rearrange("c (m e) -> c e m", e=2),
-            scalar=recip[:, 0:1],
-            in1=sx2_scaled[:],
-            op0=ALU.mult,
-            op1=ALU.add,
-        )
+        protoT_ps = psum_work.tile([P, PACK, C], F32, tag="work")
+        for e in range(2):
+            nc.vector.scalar_tensor_tensor(
+                out=proto[:, e, :],
+                in0=wu_ps[:].rearrange("c (m e) -> c e m", e=2)[:, e, :],
+                scalar=recip[:, 0:1],
+                in1=sx2_scaled[:, e, :],
+                op0=ALU.mult,
+                op1=ALU.add,
+            )
+            for u in range(2):
+                nc.tensor.transpose(protoT_ps[:, 2 * u + e, :], proto[:, e, u * P : (u + 1) * P], ident[:])
         p2 = keep.tile([P, 1], F32)
         proto_sq = keep.tile([P, 2, D // 2], F32)
         nc.scalar.activation(out=proto_sq[:], in_=proto[:], func=ACT.Square, accum_out=p2[:, 0:1])
-        query_norm(late + 2)
-        query_quantise(2 * QUARTER)
         query_regroup(nc.vector.tensor_copy, late)
+        query_regroup(nc.vector.tensor_copy, late + 2)
+        query_transposes(late + QUARTER)
+        query_transposes(late + QUARTER + 2)
+        for t in range(late + QUARTER, Q_TILES - 1):
+            query_norm(t)
 
-        protoT_ps = psum_work.tile([P, PACK, C], F32, tag="work")
-        for u in range(2):
-            for e in range(2):
-                nc.tensor.transpose(protoT_ps[:, 2 * u + e, :], proto[:, e, u * P : (u + 1) * P], ident[:])
         p2_ps = psum_work.tile([P, D], F32, tag="work")
         nc.tensor.matmul(
             out=p2_ps[:, 0:C], lhsT=p2[:, 0:1].to_broadcast([P, P]), rhs=ident[:], start=True, stop=True
         )
         neg_p2_rows = keep.tile([P, C], F32)
         nc.scalar.mul(out=neg_p2_rows[:], in_=p2_ps[:, 0:C], mul=-1.0)
-        query_norm(late + 3)
+        query_norm(Q_TILES - 1)
 
         p_grouped = keep.tile([P, C, PACK], BF16, align_bytes=64)
         nc.vector.tensor_scalar_mul(
@@ -328,8 +333,10 @@ def tile_proto_metric_semi_k_kernel(tc, x1, x2, x3, w, out):
             scales=p_scales[:],
             in_=p_grouped[:].rearrange("p c t -> p (c t)"),
         )
-        query_regroup(nc.vector.tensor_copy, late + 2)
+        query_regroup(nc.vector.tensor_copy, late + QUARTER)
+        query_regroup(nc.vector.tensor_copy, late + QUARTER + 2)
         query_quantise(late)
+        query_quantise(late + QUARTER)
 
         cross_ps = [psum_work.tile([P, QUARTER, C], F32, name="cross_ps", tag="work") for b in range(4)]
         for b in range(4):

@@ -20,6 +20,8 @@ PASSES = U // K_PASS
 ROUND_PASSES = 2
 ROUNDS = PASSES // ROUND_PASSES
 RAW_BUFS = 6
+RAW_GROUPS = 4
+RUN = 16
 W_GROUP_PASSES = 4
 W_GROUPS = PASSES // W_GROUP_PASSES
 Q_TILES = B // P
@@ -44,15 +46,16 @@ def regroup(copy, grouped, rows):
 def tile_proto_metric_semi_k_kernel(tc, x1, x2, x3, w, out):
     nc = tc.nc
 
-    x3_view = x3.rearrange("(g p j) d -> p g j d", p=P, j=PACK)
-    w_view = w.rearrange("(g p j) c -> p g j c", p=P, j=PACK)
+    x3_view = x3.rearrange("(h n c q l) d -> h c q n l d", h=2, c=4, q=2, l=RUN)
+    w_view = w.rearrange("(h n c q l) k -> h c q n l k", h=2, c=4, q=2, l=RUN)
     x2_view = x2.rearrange("c s d -> (c s) d").rearrange("(k p e) d -> p k e d", p=P, e=PACK)
     x1_view = x1.rearrange("(p t) d a b -> p t (d a b)", t=Q_TILES)
     out_view = out.rearrange("(p t) c -> p t c", t=Q_TILES)
 
     with ExitStack() as stack:
         keep = stack.enter_context(tc.tile_pool(name="keep", bufs=1))
-        raw = stack.enter_context(tc.tile_pool(name="raw", bufs=RAW_BUFS))
+        raw = stack.enter_context(tc.tile_pool(name="raw", bufs=RAW_GROUPS))
+        w_pool = stack.enter_context(tc.tile_pool(name="w_pool", bufs=4))
         stage = stack.enter_context(tc.tile_pool(name="stage", bufs=4))
         w_stage = stack.enter_context(tc.tile_pool(name="w_stage", bufs=2))
         psum_keep = stack.enter_context(tc.psum_pool(name="psum_keep", bufs=1))
@@ -73,7 +76,6 @@ def tile_proto_metric_semi_k_kernel(tc, x1, x2, x3, w, out):
         class_of_row = keep.tile([P, X2_CLASSES], BF16)
         nc.vector.tensor_copy(out=class_of_row[:], in_=class_of_row_f32[:])
 
-        w_raw = [keep.tile([P, W_GROUP_PASSES, PACK, C], BF16, name="w_raw%d" % a) for a in range(W_GROUPS)]
         w_codes = keep.tile([P, PASSES, C], U32, align_bytes=64)
         w_scales = keep.tile([P, PASSES, C], U8, align_bytes=64)
         x2_raw = keep.tile([P, X2_TILES, PACK, D], BF16)
@@ -87,26 +89,32 @@ def tile_proto_metric_semi_k_kernel(tc, x1, x2, x3, w, out):
         den_ps = psum_keep.tile([P, D], F32)
         sx2T_ps = psum_keep.tile([P, D // P, C], F32)
 
-        x3_raw, x3_grouped, x3_codes, x3_scales, w_grouped, qT_ps = {}, {}, {}, {}, {}, {}
+        x3_raw, x3_grouped, x3_codes, x3_scales, w_raw, w_grouped, qT_ps = {}, {}, {}, {}, {}, {}, {}
 
         def load_w(a):
-            g0 = a * W_GROUP_PASSES
-            nc.sync.dma_start(out=w_raw[a][:], in_=w_view[:, g0 : g0 + W_GROUP_PASSES])
+            w_raw[a] = w_pool.tile([P, RUN, C], BF16, name="w_raw")
+            for q in range(2):
+                nc.sync.dma_start(out=w_raw[a][q:P:2], in_=w_view[a // 4, a % 4, q])
+
+        def load_rows(a, l0, l1):
+            for q in range(2):
+                nc.sync.dma_start(out=x3_raw[a][q:P:2, l0:l1], in_=x3_view[a // 4, a % 4, q, :, l0:l1])
 
         def load_queries(quarter):
             t0 = quarter * QUARTER
             nc.sync.dma_start(out=q_raw[:, t0 : t0 + QUARTER, :], in_=x1_view[:, t0 : t0 + QUARTER, :])
 
         def load_round(r):
-            g0 = r * ROUND_PASSES
-            x3_raw[r] = raw.tile([P, ROUND_PASSES, PACK, D], BF16, name="x3_raw")
+            a, l0 = r // 2, (r % 2) * (RUN // 2)
+            if r % 2 == 0:
+                x3_raw[a] = raw.tile([P, RUN, D], BF16, name="x3_raw")
             if r in (0, ROUNDS - 1):
-                nc.sync.dma_start(out=x3_raw[r][:, 0:1], in_=x3_view[:, g0 : g0 + 1])
+                load_rows(a, l0, l0 + PACK)
                 if r == 0:
                     load_w(0)
-                nc.sync.dma_start(out=x3_raw[r][:, 1:2], in_=x3_view[:, g0 + 1 : g0 + 2])
+                load_rows(a, l0 + PACK, l0 + 2 * PACK)
             else:
-                nc.sync.dma_start(out=x3_raw[r][:], in_=x3_view[:, g0 : g0 + ROUND_PASSES])
+                load_rows(a, l0, l0 + 2 * PACK)
             if r % 2 == 1 and (r + 1) // 2 < W_GROUPS:
                 load_w((r + 1) // 2)
             if r % 2 == 0:
@@ -121,7 +129,8 @@ def tile_proto_metric_semi_k_kernel(tc, x1, x2, x3, w, out):
                     load_queries(quarter)
 
         def regroup_pass(g, vector_cols):
-            rows = x3_raw[g // ROUND_PASSES][:, g % ROUND_PASSES]
+            l0 = (g % W_GROUP_PASSES) * PACK
+            rows = x3_raw[g // W_GROUP_PASSES][:, l0 : l0 + PACK]
             x3_grouped[g] = stage.tile([P, D, PACK], BF16, align_bytes=64, name="x3_grouped")
             if vector_cols > 0:
                 regroup(nc.vector.tensor_copy, x3_grouped[g][:, 0:vector_cols, :], rows[:, :, 0:vector_cols])
@@ -152,7 +161,7 @@ def tile_proto_metric_semi_k_kernel(tc, x1, x2, x3, w, out):
             w_grouped[a] = w_stage.tile([P, W_GROUP_PASSES, C, PACK], BF16, align_bytes=64, name="w_grouped")
             nc.vector.tensor_copy(
                 out=w_grouped[a][:].rearrange("p g (c i) j -> p g c j i", i=4),
-                in_=w_raw[a][:].rearrange("p g j (c i) -> p g c j i", i=4),
+                in_=w_raw[a][:].rearrange("p (g j) (c i) -> p g c j i", j=PACK, i=4),
             )
 
         def quantise_w(a):
@@ -168,7 +177,7 @@ def tile_proto_metric_semi_k_kernel(tc, x1, x2, x3, w, out):
                 for j in range(PACK):
                     nc.tensor.matmul(
                         out=den_ps[:, 0:ONES_COLS],
-                        lhsT=w_raw[a][:, g, j, :],
+                        lhsT=w_raw[a][:, g * PACK + j, :],
                         rhs=ones[:],
                         start=(a == 0 and g == 0 and j == 0),
                         stop=(a == W_GROUPS - 1 and g == W_GROUP_PASSES - 1 and j == PACK - 1),

@@ -20,7 +20,6 @@ PASSES = U // K_PASS
 ROUND_PASSES = 2
 ROUNDS = PASSES // ROUND_PASSES
 RAW_BUFS = 6
-RAW_GROUPS = 4
 RUN = 16
 W_GROUP_PASSES = 4
 W_GROUPS = PASSES // W_GROUP_PASSES
@@ -54,7 +53,8 @@ def tile_proto_metric_semi_k_kernel(tc, x1, x2, x3, w, out):
 
     with ExitStack() as stack:
         keep = stack.enter_context(tc.tile_pool(name="keep", bufs=1))
-        raw = stack.enter_context(tc.tile_pool(name="raw", bufs=RAW_GROUPS))
+        raw = stack.enter_context(tc.tile_pool(name="raw", bufs=RAW_BUFS))
+        raw_pass = stack.enter_context(tc.tile_pool(name="raw_pass", bufs=2))
         w_pool = stack.enter_context(tc.tile_pool(name="w_pool", bufs=4))
         stage = stack.enter_context(tc.tile_pool(name="stage", bufs=4))
         w_stage = stack.enter_context(tc.tile_pool(name="w_stage", bufs=2))
@@ -96,25 +96,28 @@ def tile_proto_metric_semi_k_kernel(tc, x1, x2, x3, w, out):
             for q in range(2):
                 nc.sync.dma_start(out=w_raw[a][q:P:2], in_=w_view[a // 4, a % 4, q])
 
-        def load_rows(a, l0, l1):
+        def load_passes(g, count):
+            pool = raw if count > 1 else raw_pass
+            rows = pool.tile([P, count * PACK, D], BF16, name="x3_raw%d" % count)
+            a, l0 = g // W_GROUP_PASSES, (g % W_GROUP_PASSES) * PACK
             for q in range(2):
-                nc.sync.dma_start(out=x3_raw[a][q:P:2, l0:l1], in_=x3_view[a // 4, a % 4, q, :, l0:l1])
+                nc.sync.dma_start(out=rows[q:P:2], in_=x3_view[a // 4, a % 4, q, :, l0 : l0 + count * PACK])
+            for i in range(count):
+                x3_raw[g + i] = rows[:, i * PACK : (i + 1) * PACK]
 
         def load_queries(quarter):
             t0 = quarter * QUARTER
             nc.sync.dma_start(out=q_raw[:, t0 : t0 + QUARTER, :], in_=x1_view[:, t0 : t0 + QUARTER, :])
 
         def load_round(r):
-            a, l0 = r // 2, (r % 2) * (RUN // 2)
-            if r % 2 == 0:
-                x3_raw[a] = raw.tile([P, RUN, D], BF16, name="x3_raw")
+            g0 = r * ROUND_PASSES
             if r in (0, ROUNDS - 1):
-                load_rows(a, l0, l0 + PACK)
+                load_passes(g0, 1)
                 if r == 0:
                     load_w(0)
-                load_rows(a, l0 + PACK, l0 + 2 * PACK)
+                load_passes(g0 + 1, 1)
             else:
-                load_rows(a, l0, l0 + 2 * PACK)
+                load_passes(g0, ROUND_PASSES)
             if r % 2 == 1 and (r + 1) // 2 < W_GROUPS:
                 load_w((r + 1) // 2)
             if r % 2 == 0:
@@ -129,8 +132,7 @@ def tile_proto_metric_semi_k_kernel(tc, x1, x2, x3, w, out):
                     load_queries(quarter)
 
         def regroup_pass(g, vector_cols):
-            l0 = (g % W_GROUP_PASSES) * PACK
-            rows = x3_raw[g // W_GROUP_PASSES][:, l0 : l0 + PACK]
+            rows = x3_raw[g]
             x3_grouped[g] = stage.tile([P, D, PACK], BF16, align_bytes=64, name="x3_grouped")
             if vector_cols > 0:
                 regroup(nc.vector.tensor_copy, x3_grouped[g][:, 0:vector_cols, :], rows[:, :, 0:vector_cols])

@@ -32,7 +32,32 @@ X2_CLASSES = C // X2_TILES
 SHARED_VECTOR_COLS = 336
 SCALAR_BANK = 1
 
+X2_ROUNDS = (9, 10, 11, 12)
+Q_ROUNDS = (0, 2, 15, 15)
+COLS = (248, 112, 376, 240)
+DEN_SLOT = 29
+W_SLOT0 = 8
+CODE_BUFS = 10
+LAG = 2
+
 FLOPS = 2 * U * C * D + 2 * B * D * C
+
+
+def w_round(a):
+    return a + (W_SLOT0 - 2) // 2
+
+
+def vector_cols(n):
+    norms = any(2 * r + 3 <= n < 2 * r + 8 for r in Q_ROUNDS)
+    return COLS[(1 if W_SLOT0 <= n < W_SLOT0 + 16 else 0) + (2 if norms else 0)]
+
+
+def w_slot(a):
+    return 2 * a + W_SLOT0
+
+
+def vector_owns(n):
+    return n * 7 % 16 < 7
 
 
 def regroup(copy, grouped, rows):
@@ -56,6 +81,8 @@ def tile_proto_metric_semi_k_kernel(tc, x1, x2, x3, w, out):
         raw = stack.enter_context(tc.tile_pool(name="raw", bufs=RAW_BUFS))
         raw_pass = stack.enter_context(tc.tile_pool(name="raw_pass", bufs=2))
         w_pool = stack.enter_context(tc.tile_pool(name="w_pool", bufs=4))
+        grouped = stack.enter_context(tc.tile_pool(name="grouped", bufs=5))
+        codes = stack.enter_context(tc.tile_pool(name="codes", bufs=CODE_BUFS))
         stage = stack.enter_context(tc.tile_pool(name="stage", bufs=4))
         w_stage = stack.enter_context(tc.tile_pool(name="w_stage", bufs=2))
         psum_keep = stack.enter_context(tc.psum_pool(name="psum_keep", bufs=1))
@@ -75,6 +102,9 @@ def tile_proto_metric_semi_k_kernel(tc, x1, x2, x3, w, out):
         )
         class_of_row = keep.tile([P, X2_CLASSES], BF16)
         nc.vector.tensor_copy(out=class_of_row[:], in_=class_of_row_f32[:])
+
+        warm = keep.tile([P, 1], F32)
+        nc.scalar.activation(out=warm[:], in_=ones[:, 0:1], func=ACT.Square)
 
         w_codes = keep.tile([P, PASSES, C], U32, align_bytes=64)
         w_scales = keep.tile([P, PASSES, C], U8, align_bytes=64)
@@ -110,38 +140,32 @@ def tile_proto_metric_semi_k_kernel(tc, x1, x2, x3, w, out):
             nc.sync.dma_start(out=q_raw[:, t0 : t0 + QUARTER, :], in_=x1_view[:, t0 : t0 + QUARTER, :])
 
         def load_round(r):
-            g0 = r * ROUND_PASSES
             if r in (0, ROUNDS - 1):
-                load_passes(g0, 1)
-                if r == 0:
-                    load_w(0)
-                load_passes(g0 + 1, 1)
+                load_passes(2 * r, 1)
+                load_passes(2 * r + 1, 1)
             else:
-                load_passes(g0, ROUND_PASSES)
-            if r % 2 == 1 and (r + 1) // 2 < W_GROUPS:
-                load_w((r + 1) // 2)
-            if r % 2 == 0:
-                piece = r // 2
-                if piece < EARLY_QUARTERS:
-                    load_queries(piece)
-                elif piece < EARLY_QUARTERS + X2_TILES:
-                    k = piece - EARLY_QUARTERS
+                load_passes(2 * r, 2)
+            for a in range(W_GROUPS):
+                if r == w_round(a):
+                    load_w(a)
+            for k in range(X2_TILES):
+                if r == X2_ROUNDS[k]:
                     nc.sync.dma_start(out=x2_raw[:, k], in_=x2_view[:, k])
-            if r == ROUNDS - 1:
-                for quarter in range(EARLY_QUARTERS, Q_TILES // QUARTER):
+            for quarter in range(Q_TILES // QUARTER):
+                if r == Q_ROUNDS[quarter]:
                     load_queries(quarter)
 
         def regroup_pass(g, vector_cols):
             rows = x3_raw[g]
-            x3_grouped[g] = stage.tile([P, D, PACK], BF16, align_bytes=64, name="x3_grouped")
+            x3_grouped[g] = grouped.tile([P, D, PACK], BF16, align_bytes=64, name="x3_grouped")
             if vector_cols > 0:
                 regroup(nc.vector.tensor_copy, x3_grouped[g][:, 0:vector_cols, :], rows[:, :, 0:vector_cols])
             if vector_cols < D:
                 regroup(nc.scalar.copy, x3_grouped[g][:, vector_cols:D, :], rows[:, :, vector_cols:D])
 
         def quantise_pass(g):
-            x3_codes[g] = stage.tile([P, D], U32, align_bytes=64, name="x3_codes")
-            x3_scales[g] = stage.tile([P, D], U8, align_bytes=64, name="x3_scales")
+            x3_codes[g] = codes.tile([P, D], U32, align_bytes=64, name="x3_codes")
+            x3_scales[g] = codes.tile([P, D], U8, align_bytes=64, name="x3_scales")
             nc.vector.quantize_mx(
                 out=x3_codes[g][:].bitcast(FP8X4),
                 scales=x3_scales[g][:],
@@ -248,59 +272,63 @@ def tile_proto_metric_semi_k_kernel(tc, x1, x2, x3, w, out):
 
         for r in range(RAW_BUFS):
             load_round(r)
-
-        early_tiles = EARLY_QUARTERS * QUARTER
-        last_support_round = 2 * (EARLY_QUARTERS + X2_TILES) - 1
-        last_w_round = 2 * (W_GROUPS - 1) - 1
-        for r in range(ROUNDS - 1):
-            t = r - 1
-            if r == last_support_round + 1:
-                sx2_ps = transpose_support_sums()
-            if 0 <= t < early_tiles and t % 2 == 1:
-                query_transposes(t - 1)
-            regroup_pass(2 * r, D)
-            regroup_pass(2 * r + 1, 0)
-            if r + RAW_BUFS < ROUNDS:
-                load_round(r + RAW_BUFS)
-            if r > 0:
-                quantise_pass(2 * r - 1)
-                multiply_pass(2 * r - 1)
-            a = (r + 1) // 2
-            prepares_w = (r == 0 or r % 2 == 1) and a < W_GROUPS
-            if prepares_w:
-                regroup_w(a)
-            quantise_pass(2 * r)
-            if prepares_w:
-                quantise_w(a)
-                sum_w(a)
-            multiply_pass(2 * r)
-            if 0 <= t < early_tiles:
-                query_norm(t)
-                if t % 2 == 1:
-                    query_regroup(nc.scalar.copy, t - 1)
-            k = (r - 1) // 2 - EARLY_QUARTERS
-            if r % 2 == 1 and 0 <= k < X2_TILES:
-                support_tile(k)
-            if r == last_w_round:
-                finish_denominator()
-            if r == last_w_round + 1:
-                scale_support_sums(sx2_ps)
-
+        sx2_ps = []
         late = EARLY_QUARTERS * QUARTER
-        regroup_pass(PASSES - 2, SHARED_VECTOR_COLS)
-        quantise_pass(PASSES - 3)
-        multiply_pass(PASSES - 3)
-        regroup_pass(PASSES - 1, SHARED_VECTOR_COLS)
-        quantise_pass(PASSES - 2)
-        multiply_pass(PASSES - 2)
-        quantise_pass(PASSES - 1)
-        multiply_pass(PASSES - 1)
-        query_transposes(late)
-        query_transposes(late + 2)
-        for t in range(late, late + QUARTER):
+        early_tiles = [t for t in range(Q_TILES) if Q_ROUNDS[t // QUARTER] < ROUNDS - 1]
+
+        def side_work(p):
+            for quarter in range(Q_TILES // QUARTER):
+                first = 2 * Q_ROUNDS[quarter] + 3
+                t0 = quarter * QUARTER
+                if Q_ROUNDS[quarter] < ROUNDS - 1:
+                    i = p - first
+                    if 0 <= i < QUARTER:
+                        query_norm(t0 + i)
+                    if i in (1, 3):
+                        query_transposes(t0 + i - 1)
+                    if i in (2, 4):
+                        query_regroup(nc.scalar.copy, t0 + i - 2)
+                    if i == 5:
+                        query_quantise(t0)
+            for k in range(X2_TILES):
+                if p == 2 * X2_ROUNDS[k] + 3:
+                    support_tile(k)
+            if p == 2 * X2_ROUNDS[-1] + 4:
+                sx2_ps.append(transpose_support_sums())
+            if p == PASSES - 1:
+                query_transposes(late)
+                query_transposes(late + 2)
+            if p == DEN_SLOT:
+                finish_denominator()
+            if p == DEN_SLOT + 1:
+                scale_support_sums(sx2_ps[0])
+
+        multiplied = 0
+        for n in range(PASSES + LAG):
+            p = n - LAG
+            if p >= 0 and n < PASSES:
+                quantise_pass(p)
+            if n < PASSES:
+                shared = n < 2 or n >= PASSES - 2
+                regroup_pass(n, SHARED_VECTOR_COLS if shared else vector_cols(n))
+                if n % 2 == 1 and n // 2 + RAW_BUFS < ROUNDS:
+                    load_round(n // 2 + RAW_BUFS)
+            elif p >= 0:
+                quantise_pass(p)
+            for a in range(W_GROUPS):
+                if n == w_slot(a):
+                    regroup_w(a)
+                if n == w_slot(a) + 1:
+                    quantise_w(a)
+                    sum_w(a)
+            while multiplied <= p and (n >= w_slot(0) + 1) and n >= w_slot(multiplied // 4) + 1:
+                multiply_pass(multiplied)
+                multiplied += 1
+            side_work(n)
+
+        query_regroup(nc.vector.tensor_copy, late)
+        for t in range(late, late + 3):
             query_norm(t)
-        query_quantise(0)
-        query_quantise(QUARTER)
 
         proto = keep.tile([P, 2, D // 2], F32)
         protoT_ps = psum_work.tile([P, PACK, C], F32, tag="work")
@@ -318,12 +346,10 @@ def tile_proto_metric_semi_k_kernel(tc, x1, x2, x3, w, out):
         p2 = keep.tile([P, 1], F32)
         proto_sq = keep.tile([P, 2, D // 2], F32)
         nc.scalar.activation(out=proto_sq[:], in_=proto[:], func=ACT.Square, accum_out=p2[:, 0:1])
-        query_regroup(nc.vector.tensor_copy, late)
-        query_regroup(nc.vector.tensor_copy, late + 2)
         query_transposes(late + QUARTER)
         query_transposes(late + QUARTER + 2)
-        for t in range(late + QUARTER, Q_TILES - 1):
-            query_norm(t)
+        query_regroup(nc.vector.tensor_copy, late + 2)
+        query_norm(late + 3)
 
         p2_ps = psum_work.tile([P, D], F32, tag="work")
         nc.tensor.matmul(
@@ -331,7 +357,7 @@ def tile_proto_metric_semi_k_kernel(tc, x1, x2, x3, w, out):
         )
         neg_p2_rows = keep.tile([P, C], F32)
         nc.scalar.mul(out=neg_p2_rows[:], in_=p2_ps[:, 0:C], mul=-1.0)
-        query_norm(Q_TILES - 1)
+        query_regroup(nc.scalar.copy, late + QUARTER)
 
         p_grouped = keep.tile([P, C, PACK], BF16, align_bytes=64)
         nc.vector.tensor_scalar_mul(
@@ -344,13 +370,13 @@ def tile_proto_metric_semi_k_kernel(tc, x1, x2, x3, w, out):
             scales=p_scales[:],
             in_=p_grouped[:].rearrange("p c t -> p (c t)"),
         )
-        query_regroup(nc.vector.tensor_copy, late + QUARTER)
         query_regroup(nc.vector.tensor_copy, late + QUARTER + 2)
         query_quantise(late)
-        query_quantise(late + QUARTER)
 
-        cross_ps = [psum_work.tile([P, QUARTER, C], F32, name="cross_ps", tag="work") for b in range(4)]
-        for b in range(4):
+        cross_ps = {}
+
+        def cross_bank(b):
+            cross_ps[b] = psum_work.tile([P, QUARTER, C], F32, name="cross_ps", tag="work")
             for tt in range(QUARTER):
                 nc.tensor.matmul_mx(
                     out=cross_ps[b][:, tt, :],
@@ -389,5 +415,14 @@ def tile_proto_metric_semi_k_kernel(tc, x1, x2, x3, w, out):
             t0 = b * QUARTER
             nc.sync.dma_start(out=out_view[:, t0 : t0 + QUARTER, :], in_=out_sb[:, t0 : t0 + QUARTER, :])
 
-        for b in (0, 2, SCALAR_BANK, 3):
-            finish_bank(b)
+        cross_bank(0)
+        cross_bank(1)
+        cross_bank(2)
+        finish_bank(0)
+        query_quantise(late + QUARTER)
+        cross_bank(3)
+        finish_bank(SCALAR_BANK)
+        for t in range(late + QUARTER, Q_TILES):
+            query_norm(t)
+        finish_bank(2)
+        finish_bank(3)

@@ -19,7 +19,7 @@ B, D, C, SHOT, U = 2048, 512, 128, 16, 16384
 PASSES = U // K_PASS
 ROUND_PASSES = 2
 ROUNDS = PASSES // ROUND_PASSES
-RAW_BUFS = 6
+RAW_BUFS = 5
 RUN = 16
 W_GROUP_PASSES = 4
 W_GROUPS = PASSES // W_GROUP_PASSES
@@ -33,11 +33,14 @@ SHARED_VECTOR_COLS = 336
 SCALAR_BANK = 1
 
 X2_ROUNDS = (9, 10, 11, 12)
-Q_ROUNDS = (0, 2, 15, 15)
-COLS = (248, 112, 376, 240)
-DEN_SLOT = 29
-W_SLOT0 = 8
-CODE_BUFS = 10
+Q_ROUNDS = (6, 8, 15, 15)
+COLS = (240, 128, 368, 240)
+DEN_SLOT = 26
+SX2_SLOT = 30
+FINE = 12
+SCALE_SLOT = 32
+W_SLOT0 = 4
+CODE_BUFS = 7
 LAG = 2
 
 FLOPS = 2 * U * C * D + 2 * B * D * C
@@ -79,7 +82,7 @@ def tile_proto_metric_semi_k_kernel(tc, x1, x2, x3, w, out):
     with ExitStack() as stack:
         keep = stack.enter_context(tc.tile_pool(name="keep", bufs=1))
         raw = stack.enter_context(tc.tile_pool(name="raw", bufs=RAW_BUFS))
-        raw_pass = stack.enter_context(tc.tile_pool(name="raw_pass", bufs=2))
+        raw_pass = stack.enter_context(tc.tile_pool(name="raw_pass", bufs=6))
         w_pool = stack.enter_context(tc.tile_pool(name="w_pool", bufs=4))
         grouped = stack.enter_context(tc.tile_pool(name="grouped", bufs=5))
         codes = stack.enter_context(tc.tile_pool(name="codes", bufs=CODE_BUFS))
@@ -140,7 +143,7 @@ def tile_proto_metric_semi_k_kernel(tc, x1, x2, x3, w, out):
             nc.sync.dma_start(out=q_raw[:, t0 : t0 + QUARTER, :], in_=x1_view[:, t0 : t0 + QUARTER, :])
 
         def load_round(r):
-            if r in (0, ROUNDS - 1):
+            if r == 0 or r >= FINE:
                 load_passes(2 * r, 1)
                 load_passes(2 * r + 1, 1)
             else:
@@ -293,14 +296,14 @@ def tile_proto_metric_semi_k_kernel(tc, x1, x2, x3, w, out):
             for k in range(X2_TILES):
                 if p == 2 * X2_ROUNDS[k] + 3:
                     support_tile(k)
-            if p == 2 * X2_ROUNDS[-1] + 4:
+            if p == SX2_SLOT:
                 sx2_ps.append(transpose_support_sums())
             if p == PASSES - 1:
                 query_transposes(late)
                 query_transposes(late + 2)
             if p == DEN_SLOT:
                 finish_denominator()
-            if p == DEN_SLOT + 1:
+            if p == SCALE_SLOT:
                 scale_support_sums(sx2_ps[0])
 
         multiplied = 0

@@ -30,17 +30,20 @@ ONES_COLS = 32
 X2_TILES = C * SHOT // K_PASS
 X2_CLASSES = C // X2_TILES
 SHARED_VECTOR_COLS = 336
+SCALAR_TILES = 2
 SCALAR_BANK = 1
 
-X2_ROUNDS = (9, 10, 11, 12)
-Q_ROUNDS = (6, 8, 15, 15)
-COLS = (240, 128, 368, 240)
+X2_ROUNDS = (10, 11, 12, 13)
+Q_ROUNDS = (0, 8, 15, 15)
+COLS = (248, 112, 368, 240)
 DEN_SLOT = 26
 SX2_SLOT = 30
-FINE = 12
+FINE = 13
+HEAD = 2
 SCALE_SLOT = 32
-W_SLOT0 = 4
-CODE_BUFS = 7
+W_SLOT0 = 8
+STORES = ((3,), (3,), (3,), (1, 3))
+CODE_BUFS = 9
 LAG = 2
 
 FLOPS = 2 * U * C * D + 2 * B * D * C
@@ -65,8 +68,8 @@ def vector_owns(n):
 
 def regroup(copy, grouped, rows):
     copy(
-        out=grouped.rearrange("p (c i) j -> p c j i", i=4),
-        in_=rows.rearrange("p j (c i) -> p c j i", i=4),
+        out=grouped.rearrange("p (c i) j -> p c j i", i=8),
+        in_=rows.rearrange("p j (c i) -> p c j i", i=8),
     )
 
 
@@ -143,7 +146,7 @@ def tile_proto_metric_semi_k_kernel(tc, x1, x2, x3, w, out):
             nc.sync.dma_start(out=q_raw[:, t0 : t0 + QUARTER, :], in_=x1_view[:, t0 : t0 + QUARTER, :])
 
         def load_round(r):
-            if r == 0 or r >= FINE:
+            if r <= HEAD or r >= FINE:
                 load_passes(2 * r, 1)
                 load_passes(2 * r + 1, 1)
             else:
@@ -189,8 +192,8 @@ def tile_proto_metric_semi_k_kernel(tc, x1, x2, x3, w, out):
         def regroup_w(a):
             w_grouped[a] = w_stage.tile([P, W_GROUP_PASSES, C, PACK], BF16, align_bytes=64, name="w_grouped")
             nc.vector.tensor_copy(
-                out=w_grouped[a][:].rearrange("p g (c i) j -> p g c j i", i=4),
-                in_=w_raw[a][:].rearrange("p (g j) (c i) -> p g c j i", j=PACK, i=4),
+                out=w_grouped[a][:].rearrange("p g (c i) j -> p g c j i", i=8),
+                in_=w_raw[a][:].rearrange("p (g j) (c i) -> p g c j i", j=PACK, i=8),
             )
 
         def quantise_w(a):
@@ -392,9 +395,10 @@ def tile_proto_metric_semi_k_kernel(tc, x1, x2, x3, w, out):
                 )
 
         def finish_bank(b):
+            t0 = b * QUARTER
             for tt in range(QUARTER):
                 t = b * QUARTER + tt
-                if b == SCALAR_BANK:
+                if b == SCALAR_BANK and tt < SCALAR_TILES:
                     q2_minus_cross = stage.tile([P, C], F32)
                     nc.scalar.activation(
                         out=q2_minus_cross[:],
@@ -415,8 +419,9 @@ def tile_proto_metric_semi_k_kernel(tc, x1, x2, x3, w, out):
                         op0=ALU.subtract,
                         op1=ALU.add,
                     )
-            t0 = b * QUARTER
-            nc.sync.dma_start(out=out_view[:, t0 : t0 + QUARTER, :], in_=out_sb[:, t0 : t0 + QUARTER, :])
+                if tt in STORES[b]:
+                    nc.sync.dma_start(out=out_view[:, t0 : t + 1, :], in_=out_sb[:, t0 : t + 1, :])
+                    t0 = t + 1
 
         cross_bank(0)
         cross_bank(1)

@@ -26,7 +26,8 @@ W_GROUPS = PASSES // W_GROUP_PASSES
 Q_TILES = B // P
 QUARTER = Q_TILES // 4
 EARLY_QUARTERS = 2
-ONES_COLS = 32
+WARM = (27, 28, 29, 30)
+ONES_COLS = 16
 X2_TILES = C * SHOT // K_PASS
 X2_CLASSES = C // X2_TILES
 SHARED_VECTOR_COLS = 336
@@ -215,6 +216,10 @@ def tile_proto_metric_semi_k_kernel(tc, x1, x2, x3, w, out):
                         stop=(a == W_GROUPS - 1 and g == W_GROUP_PASSES - 1 and j == PACK - 1),
                     )
 
+        def keep_warm(cols):
+            sample = w_raw[W_GROUPS - 1][:, 0 : cols // C, :].rearrange("p r k -> p (r k)")
+            nc.tensor.matmul(out=den_ps[:, 0:cols], lhsT=w_raw[W_GROUPS - 1][:, 0, :], rhs=sample, start=True, stop=True)
+
         def query_norm(t):
             sq_junk = stage.tile([P, D], BF16)
             nc.scalar.activation(
@@ -329,6 +334,8 @@ def tile_proto_metric_semi_k_kernel(tc, x1, x2, x3, w, out):
                     sum_w(a)
             while multiplied <= p and (n >= w_slot(0) + 1) and n >= w_slot(multiplied // 4) + 1:
                 multiply_pass(multiplied)
+                if multiplied in WARM:
+                    keep_warm(256)
                 multiplied += 1
             side_work(n)
 
@@ -354,6 +361,7 @@ def tile_proto_metric_semi_k_kernel(tc, x1, x2, x3, w, out):
         nc.scalar.activation(out=proto_sq[:], in_=proto[:], func=ACT.Square, accum_out=p2[:, 0:1])
         query_transposes(late + QUARTER)
         query_transposes(late + QUARTER + 2)
+        keep_warm(512)
         query_regroup(nc.vector.tensor_copy, late + 2)
         query_norm(late + 3)
 

@@ -26,7 +26,7 @@ W_GROUPS = PASSES // W_GROUP_PASSES
 Q_TILES = B // P
 QUARTER = Q_TILES // 4
 EARLY_QUARTERS = 2
-WARM = (27, 28, 29, 30)
+WARM = (27, 28, 29, 30, 31)
 ONES_COLS = 16
 X2_TILES = C * SHOT // K_PASS
 X2_CLASSES = C // X2_TILES
@@ -34,15 +34,16 @@ SHARED_VECTOR_COLS = 336
 SCALAR_TILES = 2
 SCALAR_BANK = 1
 
-X2_ROUNDS = (10, 11, 12, 13)
-Q_ROUNDS = (0, 8, 15, 15)
-COLS = (248, 112, 368, 240)
+X2_ROUNDS = (9, 10, 11, 12)
+Q_ROUNDS = (0, 6, 15, 15)
+COLS = (240, 112, 368, 240)
 DEN_SLOT = 26
 SX2_SLOT = 30
 FINE = 13
 HEAD = 2
 SCALE_SLOT = 32
 W_SLOT0 = 8
+AHEAD = 2
 STORES = ((3,), (3,), (3,), (1, 3))
 CODE_BUFS = 9
 LAG = 2
@@ -293,7 +294,9 @@ def tile_proto_metric_semi_k_kernel(tc, x1, x2, x3, w, out):
                 t0 = quarter * QUARTER
                 if Q_ROUNDS[quarter] < ROUNDS - 1:
                     i = p - first
-                    if 0 <= i < QUARTER:
+                    if quarter == 0 and 0 <= i < QUARTER - AHEAD:
+                        query_norm(AHEAD + i)
+                    if quarter > 0 and 0 <= i < QUARTER:
                         query_norm(t0 + i)
                     if i in (1, 3):
                         query_transposes(t0 + i - 1)
@@ -317,7 +320,12 @@ def tile_proto_metric_semi_k_kernel(tc, x1, x2, x3, w, out):
         multiplied = 0
         for n in range(PASSES + LAG):
             p = n - LAG
-            if p >= 0 and n < PASSES:
+            if n == 2:
+                quantise_pass(0)
+                quantise_pass(1)
+                for t in range(AHEAD):
+                    query_norm(t)
+            elif n > LAG + 1 and n < PASSES:
                 quantise_pass(p)
             if n < PASSES:
                 shared = n < 2 or n >= PASSES - 2

from contextlib import ExitStack

import concourse.mybir as mybir
from concourse.masks import make_identity

F32 = mybir.dt.float32
BF16 = mybir.dt.bfloat16
U32 = mybir.dt.uint32
U8 = mybir.dt.uint8
FP8X4 = mybir.dt.float8_e4m3fn_x4
ALU = mybir.AluOpType
ACT = mybir.ActivationFunctionType

P = 128
PACK = 4
K_PASS = P * PACK

B, D, C, SHOT, U = 2048, 512, 128, 16, 16384
PASSES = U // K_PASS
ROUND_PASSES = 2
ROUNDS = PASSES // ROUND_PASSES
RAW_BUFS = 5
RUN = 16
W_GROUP_PASSES = 4
W_GROUPS = PASSES // W_GROUP_PASSES
Q_TILES = B // P
QUARTER = Q_TILES // 4
EARLY_QUARTERS = 2
WARM = (27, 28, 29, 30, 31)
ONES_COLS = 16
X2_TILES = C * SHOT // K_PASS
X2_CLASSES = C // X2_TILES
SHARED_VECTOR_COLS = 336
SCALAR_TILES = 2
SCALAR_BANK = 1

X2_ROUNDS = (9, 10, 11, 12)
Q_ROUNDS = (0, 6, 15, 15)
COLS = (240, 112, 368, 240)
DEN_SLOT = 26
SX2_SLOT = 30
FINE = 13
HEAD = 2
SCALE_SLOT = 32
W_SLOT0 = 8
AHEAD = 2
STORES = ((3,), (3,), (3,), (1, 3))
CODE_BUFS = 9
LAG = 2

FLOPS = 2 * U * C * D + 2 * B * D * C


def w_round(a):
    return a + (W_SLOT0 - 2) // 2


def vector_cols(n):
    norms = any(2 * r + 3 <= n < 2 * r + 8 for r in Q_ROUNDS)
    return COLS[(1 if W_SLOT0 <= n < W_SLOT0 + 16 else 0) + (2 if norms else 0)]


def w_slot(a):
    return 2 * a + W_SLOT0


def vector_owns(n):
    return n * 7 % 16 < 7


def regroup(copy, grouped, rows):
    copy(
        out=grouped.rearrange("p (c i) j -> p c j i", i=8),
        in_=rows.rearrange("p j (c i) -> p c j i", i=8),
    )


def tile_proto_metric_semi_k_kernel(tc, x1, x2, x3, w, out):
    nc = tc.nc

    x3_view = x3.rearrange("(h n c q l) d -> h c q n l d", h=2, c=4, q=2, l=RUN)
    w_view = w.rearrange("(h n c q l) k -> h c q n l k", h=2, c=4, q=2, l=RUN)
    x2_view = x2.rearrange("c s d -> (c s) d").rearrange("(k p e) d -> p k e d", p=P, e=PACK)
    x1_view = x1.rearrange("(p t) d a b -> p t (d a b)", t=Q_TILES)
    out_view = out.rearrange("(p t) c -> p t c", t=Q_TILES)

    with ExitStack() as stack:
        keep = stack.enter_context(tc.tile_pool(name="keep", bufs=1))
        raw = stack.enter_context(tc.tile_pool(name="raw", bufs=RAW_BUFS))
        raw_pass = stack.enter_context(tc.tile_pool(name="raw_pass", bufs=6))
        w_pool = stack.enter_context(tc.tile_pool(name="w_pool", bufs=4))
        grouped = stack.enter_context(tc.tile_pool(name="grouped", bufs=5))
        codes = stack.enter_context(tc.tile_pool(name="codes", bufs=CODE_BUFS))
        stage = stack.enter_context(tc.tile_pool(name="stage", bufs=4))
        w_stage = stack.enter_context(tc.tile_pool(name="w_stage", bufs=2))
        psum_keep = stack.enter_context(tc.psum_pool(name="psum_keep", bufs=1))
        psum_work = stack.enter_context(tc.psum_pool(name="psum_work", bufs=5))
        stack.enter_context(tc.manual_schedule())

        ident = keep.tile([P, P], F32)
        make_identity(nc, ident[:])
        ones = keep.tile([P, ONES_COLS], BF16)
        nc.vector.memset(ones[:], 1.0)
        class_of_row_f32 = keep.tile([P, X2_CLASSES], F32)
        nc.vector.tensor_reduce(
            out=class_of_row_f32[:],
            in_=ident[:].rearrange("p (n e) -> p n e", e=PACK),
            axis=mybir.AxisListType.X,
            op=ALU.add,
        )
        class_of_row = keep.tile([P, X2_CLASSES], BF16)
        nc.vector.tensor_copy(out=class_of_row[:], in_=class_of_row_f32[:])

        warm = keep.tile([P, 1], F32)
        nc.scalar.activation(out=warm[:], in_=ones[:, 0:1], func=ACT.Square)

        w_codes = keep.tile([P, PASSES, C], U32, align_bytes=64)
        w_scales = keep.tile([P, PASSES, C], U8, align_bytes=64)
        x2_raw = keep.tile([P, X2_TILES, PACK, D], BF16)
        q_raw = keep.tile([P, Q_TILES, D], BF16)
        q_grouped = keep.tile([P, Q_TILES, P * PACK], BF16, align_bytes=64)
        q_codes = keep.tile([P, Q_TILES, P], U32, align_bytes=64)
        q_scales = keep.tile([P, Q_TILES, P], U8, align_bytes=64)
        q2 = keep.tile([P, Q_TILES], F32)
        out_sb = keep.tile([P, Q_TILES, C], F32)
        wu_ps = psum_keep.tile([P, D], F32)
        den_ps = psum_keep.tile([P, D], F32)
        sx2T_ps = psum_keep.tile([P, D // P, C], F32)

        x3_raw, x3_grouped, x3_codes, x3_scales, w_raw, w_grouped, qT_ps = {}, {}, {}, {}, {}, {}, {}

        def load_w(a):
            w_raw[a] = w_pool.tile([P, RUN, C], BF16, name="w_raw")
            for q in range(2):
                nc.sync.dma_start(out=w_raw[a][q:P:2], in_=w_view[a // 4, a % 4, q])

        def load_passes(g, count):
            pool = raw if count > 1 else raw_pass
            rows = pool.tile([P, count * PACK, D], BF16, name="x3_raw%d" % count)
            a, l0 = g // W_GROUP_PASSES, (g % W_GROUP_PASSES) * PACK
            for q in range(2):
                nc.sync.dma_start(out=rows[q:P:2], in_=x3_view[a // 4, a % 4, q, :, l0 : l0 + count * PACK])
            for i in range(count):
                x3_raw[g + i] = rows[:, i * PACK : (i + 1) * PACK]

        def load_queries(quarter):
            t0 = quarter * QUARTER
            nc.sync.dma_start(out=q_raw[:, t0 : t0 + QUARTER, :], in_=x1_view[:, t0 : t0 + QUARTER, :])

        def load_round(r):
            if r <= HEAD or r >= FINE:
                load_passes(2 * r, 1)
                load_passes(2 * r + 1, 1)
            else:
                load_passes(2 * r, 2)
            for a in range(W_GROUPS):
                if r == w_round(a):
                    load_w(a)
            for k in range(X2_TILES):
                if r == X2_ROUNDS[k]:
                    nc.sync.dma_start(out=x2_raw[:, k], in_=x2_view[:, k])
            for quarter in range(Q_TILES // QUARTER):
                if r == Q_ROUNDS[quarter]:
                    load_queries(quarter)

        def regroup_pass(g, vector_cols):
            rows = x3_raw[g]
            x3_grouped[g] = grouped.tile([P, D, PACK], BF16, align_bytes=64, name="x3_grouped")
            if vector_cols > 0:
                regroup(nc.vector.tensor_copy, x3_grouped[g][:, 0:vector_cols, :], rows[:, :, 0:vector_cols])
            if vector_cols < D:
                regroup(nc.scalar.copy, x3_grouped[g][:, vector_cols:D, :], rows[:, :, vector_cols:D])

        def quantise_pass(g):
            x3_codes[g] = codes.tile([P, D], U32, align_bytes=64, name="x3_codes")
            x3_scales[g] = codes.tile([P, D], U8, align_bytes=64, name="x3_scales")
            nc.vector.quantize_mx(
                out=x3_codes[g][:].bitcast(FP8X4),
                scales=x3_scales[g][:],
                in_=x3_grouped[g][:].rearrange("p d j -> p (d j)"),
            )

        def multiply_pass(g):
            nc.tensor.matmul_mx(
                out=wu_ps[:],
                lhsT=w_codes[:, g, :].bitcast(FP8X4),
                lhsT_scale=w_scales[:, g, :],
                rhs=x3_codes[g][:].bitcast(FP8X4),
                rhs_scale=x3_scales[g][:],
                start=(g == 0),
                stop=(g == PASSES - 1),
            )

        def regroup_w(a):
            w_grouped[a] = w_stage.tile([P, W_GROUP_PASSES, C, PACK], BF16, align_bytes=64, name="w_grouped")
            nc.vector.tensor_copy(
                out=w_grouped[a][:].rearrange("p g (c i) j -> p g c j i", i=8),
                in_=w_raw[a][:].rearrange("p (g j) (c i) -> p g c j i", j=PACK, i=8),
            )

        def quantise_w(a):
            g0 = a * W_GROUP_PASSES
            nc.vector.quantize_mx(
                out=w_codes[:, g0 : g0 + W_GROUP_PASSES, :].rearrange("p g c -> p (g c)").bitcast(FP8X4),
                scales=w_scales[:, g0 : g0 + W_GROUP_PASSES, :].rearrange("p g c -> p (g c)"),
                in_=w_grouped[a][:].rearrange("p g c j -> p (g c j)"),
            )

        def sum_w(a):
            for g in range(W_GROUP_PASSES):
                for j in range(PACK):
                    nc.tensor.matmul(
                        out=den_ps[:, 0:ONES_COLS],
                        lhsT=w_raw[a][:, g * PACK + j, :],
                        rhs=ones[:],
                        start=(a == 0 and g == 0 and j == 0),
                        stop=(a == W_GROUPS - 1 and g == W_GROUP_PASSES - 1 and j == PACK - 1),
                    )

        def keep_warm(cols):
            sample = w_raw[W_GROUPS - 1][:, 0 : cols // C, :].rearrange("p r k -> p (r k)")
            nc.tensor.matmul(out=den_ps[:, 0:cols], lhsT=w_raw[W_GROUPS - 1][:, 0, :], rhs=sample, start=True, stop=True)

        def query_norm(t):
            sq_junk = stage.tile([P, D], BF16)
            nc.scalar.activation(
                out=sq_junk[:], in_=q_raw[:, t, :], func=ACT.Square, accum_out=q2[:, t : t + 1]
            )

        def query_transposes(t0):
            qT_ps[t0] = psum_work.tile([P, 2, 2, P], F32, name="qT_ps", tag="work")
            for tt in range(2):
                words = q_raw[:, t0 + tt, :].bitcast(F32)
                for u in range(2):
                    nc.tensor.transpose(qT_ps[t0][:, tt, u, :], words[:, u * P : (u + 1) * P], ident[:])

        def query_regroup(copy, t0):
            copy(
                out=q_grouped[:, t0 : t0 + 2, :].bitcast(F32).rearrange("p t (i u) -> p t i u", u=2),
                in_=qT_ps[t0][:].rearrange("p t u i -> p t i u"),
            )

        def query_quantise(t0):
            nc.vector.quantize_mx(
                out=q_codes[:, t0 : t0 + QUARTER, :].rearrange("p t i -> p (t i)").bitcast(FP8X4),
                scales=q_scales[:, t0 : t0 + QUARTER, :].rearrange("p t i -> p (t i)"),
                in_=q_grouped[:, t0 : t0 + QUARTER, :].rearrange("p t x -> p (t x)"),
            )

        def support_tile(k):
            for s in range(D // P):
                for e in range(PACK):
                    nc.tensor.matmul(
                        out=sx2T_ps[:, s, k * X2_CLASSES : (k + 1) * X2_CLASSES],
                        lhsT=x2_raw[:, k, e, s * P : (s + 1) * P],
                        rhs=class_of_row[:],
                        start=(e == 0),
                        stop=(e == PACK - 1),
                    )

        recip = keep.tile([P, 1], F32)
        sx2_scaled = keep.tile([P, 2, D // 2], F32)

        def finish_denominator():
            denom = keep.tile([P, 1], F32)
            nc.vector.tensor_scalar_add(out=denom[:], in0=den_ps[:, 0:1], scalar1=float(SHOT))
            nc.vector.reciprocal(out=recip[:], in_=denom[:])

        def transpose_support_sums():
            sx2T_sb = keep.tile([P, D // P, C], F32)
            nc.scalar.copy(out=sx2T_sb[:], in_=sx2T_ps[:])
            sx2_ps = psum_work.tile([P, D], F32, tag="work")
            for s in range(D // P):
                nc.tensor.transpose(sx2_ps[:, s * P : (s + 1) * P], sx2T_sb[:, s, :], ident[:])
            return sx2_ps

        def scale_support_sums(sx2_ps):
            nc.scalar.activation(
                out=sx2_scaled[:],
                in_=sx2_ps[:].rearrange("c (m e) -> c e m", e=2),
                func=ACT.Copy,
                scale=recip[:, 0:1],
            )

        for r in range(RAW_BUFS):
            load_round(r)
        sx2_ps = []
        late = EARLY_QUARTERS * QUARTER
        early_tiles = [t for t in range(Q_TILES) if Q_ROUNDS[t // QUARTER] < ROUNDS - 1]

        def side_work(p):
            for quarter in range(Q_TILES // QUARTER):
                first = 2 * Q_ROUNDS[quarter] + 3
                t0 = quarter * QUARTER
                if Q_ROUNDS[quarter] < ROUNDS - 1:
                    i = p - first
                    if quarter == 0 and 0 <= i < QUARTER - AHEAD:
                        query_norm(AHEAD + i)
                    if quarter > 0 and 0 <= i < QUARTER:
                        query_norm(t0 + i)
                    if i in (1, 3):
                        query_transposes(t0 + i - 1)
                    if i in (2, 4):
                        query_regroup(nc.scalar.copy, t0 + i - 2)
                    if i == 5:
                        query_quantise(t0)
            for k in range(X2_TILES):
                if p == 2 * X2_ROUNDS[k] + 3:
                    support_tile(k)
            if p == SX2_SLOT:
                sx2_ps.append(transpose_support_sums())
            if p == PASSES - 1:
                query_transposes(late)
                query_transposes(late + 2)
            if p == DEN_SLOT:
                finish_denominator()
            if p == SCALE_SLOT:
                scale_support_sums(sx2_ps[0])

        multiplied = 0
        for n in range(PASSES + LAG):
            p = n - LAG
            if n == 2:
                quantise_pass(0)
                quantise_pass(1)
                for t in range(AHEAD):
                    query_norm(t)
            elif n > LAG + 1 and n < PASSES:
                quantise_pass(p)
            if n < PASSES:
                shared = n < 2 or n >= PASSES - 2
                regroup_pass(n, SHARED_VECTOR_COLS if shared else vector_cols(n))
                if n % 2 == 1 and n // 2 + RAW_BUFS < ROUNDS:
                    load_round(n // 2 + RAW_BUFS)
            elif p >= 0:
                quantise_pass(p)
            for a in range(W_GROUPS):
                if n == w_slot(a):
                    regroup_w(a)
                if n == w_slot(a) + 1:
                    quantise_w(a)
                    sum_w(a)
            while multiplied <= p and (n >= w_slot(0) + 1) and n >= w_slot(multiplied // 4) + 1:
                multiply_pass(multiplied)
                if multiplied in WARM:
                    keep_warm(256)
                multiplied += 1
            side_work(n)

        query_regroup(nc.vector.tensor_copy, late)
        for t in range(late, late + 3):
            query_norm(t)

        proto = keep.tile([P, 2, D // 2], F32)
        protoT_ps = psum_work.tile([P, PACK, C], F32, tag="work")
        for e in range(2):
            nc.vector.scalar_tensor_tensor(
                out=proto[:, e, :],
                in0=wu_ps[:].rearrange("c (m e) -> c e m", e=2)[:, e, :],
                scalar=recip[:, 0:1],
                in1=sx2_scaled[:, e, :],
                op0=ALU.mult,
                op1=ALU.add,
            )
            for u in range(2):
                nc.tensor.transpose(protoT_ps[:, 2 * u + e, :], proto[:, e, u * P : (u + 1) * P], ident[:])
        p2 = keep.tile([P, 1], F32)
        proto_sq = keep.tile([P, 2, D // 2], F32)
        nc.scalar.activation(out=proto_sq[:], in_=proto[:], func=ACT.Square, accum_out=p2[:, 0:1])
        query_transposes(late + QUARTER)
        query_transposes(late + QUARTER + 2)
        keep_warm(512)
        query_regroup(nc.vector.tensor_copy, late + 2)
        query_norm(late + 3)

        p2_ps = psum_work.tile([P, D], F32, tag="work")
        nc.tensor.matmul(
            out=p2_ps[:, 0:C], lhsT=p2[:, 0:1].to_broadcast([P, P]), rhs=ident[:], start=True, stop=True
        )
        neg_p2_rows = keep.tile([P, C], F32)
        nc.scalar.mul(out=neg_p2_rows[:], in_=p2_ps[:, 0:C], mul=-1.0)
        query_regroup(nc.scalar.copy, late + QUARTER)

        p_grouped = keep.tile([P, C, PACK], BF16, align_bytes=64)
        nc.vector.tensor_scalar_mul(
            out=p_grouped[:], in0=protoT_ps[:].rearrange("p t c -> p c t"), scalar1=2.0
        )
        p_codes = keep.tile([P, C], U32, align_bytes=64)
        p_scales = keep.tile([P, C], U8, align_bytes=64)
        nc.vector.quantize_mx(
            out=p_codes[:].bitcast(FP8X4),
            scales=p_scales[:],
            in_=p_grouped[:].rearrange("p c t -> p (c t)"),
        )
        query_regroup(nc.vector.tensor_copy, late + QUARTER + 2)
        query_quantise(late)

        cross_ps = {}

        def cross_bank(b):
            cross_ps[b] = psum_work.tile([P, QUARTER, C], F32, name="cross_ps", tag="work")
            for tt in range(QUARTER):
                nc.tensor.matmul_mx(
                    out=cross_ps[b][:, tt, :],
                    lhsT=q_codes[:, b * QUARTER + tt, :].bitcast(FP8X4),
                    lhsT_scale=q_scales[:, b * QUARTER + tt, :],
                    rhs=p_codes[:].bitcast(FP8X4),
                    rhs_scale=p_scales[:],
                    start=True,
                    stop=True,
                )

        def finish_bank(b):
            t0 = b * QUARTER
            for tt in range(QUARTER):
                t = b * QUARTER + tt
                if b == SCALAR_BANK and tt < SCALAR_TILES:
                    q2_minus_cross = stage.tile([P, C], F32)
                    nc.scalar.activation(
                        out=q2_minus_cross[:],
                        in_=cross_ps[b][:, tt, :],
                        func=ACT.Identity,
                        bias=q2[:, t : t + 1],
                        scale=-1.0,
                    )
                    nc.gpsimd.tensor_tensor(
                        out=out_sb[:, t, :], in0=neg_p2_rows[:], in1=q2_minus_cross[:], op=ALU.subtract
                    )
                else:
                    nc.vector.scalar_tensor_tensor(
                        out=out_sb[:, t, :],
                        in0=cross_ps[b][:, tt, :],
                        scalar=q2[:, t : t + 1],
                        in1=neg_p2_rows[:],
                        op0=ALU.subtract,
                        op1=ALU.add,
                    )
                if tt in STORES[b]:
                    nc.sync.dma_start(out=out_view[:, t0 : t + 1, :], in_=out_sb[:, t0 : t + 1, :])
                    t0 = t + 1

        cross_bank(0)
        cross_bank(1)
        cross_bank(2)
        finish_bank(0)
        query_quantise(late + QUARTER)
        cross_bank(3)
        finish_bank(SCALAR_BANK)
        for t in range(late + QUARTER, Q_TILES):
            query_norm(t)
        finish_bank(2)
        finish_bank(3)
